import numpy as np
import ml_dtypes


def mxq(x, axis, fmt="e4m3"):
    dtype, down = {"e4m3": (ml_dtypes.float8_e4m3fn, 7), "e5m2": (ml_dtypes.float8_e5m2, 14)}[fmt]
    v = np.moveaxis(np.asarray(x, np.float32).astype(ml_dtypes.bfloat16).astype(np.float64), axis, -1)
    blocks = v.reshape(v.shape[:-1] + (-1, 32))
    amax = np.abs(blocks).max(-1, keepdims=True)
    byte = np.maximum(np.where(amax > 0, np.frexp(amax)[1] - 1 + 127, 0) - down, 1)
    scale = np.exp2(byte - 127.0)
    codes = (blocks / scale).astype(np.float32).astype(dtype).astype(np.float64)
    return np.moveaxis((codes * scale).reshape(v.shape), -1, axis)


WIDE = False


def mx_kscale(k):
    if not WIDE:
        return np.ones(k)
    levels = np.array([10, -10, 5, -5, 0])
    if k % 512:
        return np.exp2(np.random.permutation(np.resize(levels, k // 32))).repeat(32)
    a = np.empty((k // 512, 16))
    for p in range(k // 512):
        a[p, :8] = np.random.permutation(np.resize(levels, 8))
        for g in range(8):
            far = levels[np.abs(levels - a[p, g]) >= 10]
            a[p, g + 8] = far[np.random.randint(len(far))]
    return np.exp2(a.ravel()).repeat(32)


BF16 = ml_dtypes.bfloat16


def bf(x):
    return np.asarray(x, np.float32).astype(BF16)


def f64(x):
    return np.asarray(x).astype(np.float64)


B, N, VF_D, HID_D, EMB_D = 4096, 128, 512, 512, 128
C = 6.0 / np.sqrt(EMB_D)


def _partial_order_sim(hypers, hypos):
    act = np.maximum(hypers - hypos, 0.0)
    return -np.sqrt(np.sum(act * act, axis=-1))


def draw0():
    s, t = mx_kscale(VF_D), mx_kscale(HID_D)
    return {"vfs": bf(np.random.standard_normal((B, VF_D)) * s),
            "p_lfs": bf(np.random.standard_normal((B, EMB_D)) * 2.0 * C),
            "n_lfs": bf(np.random.standard_normal((N, EMB_D)) * C),
            "W_hidden": bf(np.random.standard_normal((HID_D, VF_D)) / np.sqrt(VF_D) / s[None, :] * t[:, None]),
            "b_hidden": bf(np.random.standard_normal(HID_D) * 0.5 * t),
            "W_embed": bf(np.random.standard_normal((EMB_D, HID_D)) * C / np.sqrt(HID_D) / t[None, :]),
            "b_embed": bf(np.random.standard_normal(EMB_D) * 0.5 * C)}


def core(vfs, p_lfs, n_lfs, W_hidden, b_hidden, W_embed, b_embed):
    vf_hidden = (mxq(f64(vfs), 1, "e4m3") @ mxq(f64(W_hidden), 1, "e4m3").T) + f64(b_hidden)
    vf_emb = (mxq(vf_hidden, 1, "e4m3") @ mxq(f64(W_embed), 1, "e4m3").T) + f64(b_embed)
    p_scores = _partial_order_sim(f64(p_lfs), vf_emb)
    n_scores = np.stack([_partial_order_sim(nl[None, :], vf_emb) for nl in f64(n_lfs)], axis=1)
    return np.concatenate([p_scores[:, None], n_scores], axis=1)


def e4m3fn_bytes(y):
    return np.clip(np.asarray(y, np.float64), -448.0, 448.0).astype(np.float32).astype(ml_dtypes.float8_e4m3fn).view(np.uint8)


def e4m3fn_values(b):
    return np.asarray(b, np.uint8).view(ml_dtypes.float8_e4m3fn).astype(np.float64)


def setup_inputs():
    d = draw0()
    x0 = np.asarray(d['vfs']).astype(np.float64)
    s = (np.max(np.abs(x0), axis=(0,), keepdims=True) / 448.0).astype(np.float32)
    out = {}
    for k, v in d.items():
        if k == 'vfs':
            out['vfs_bytes'] = e4m3fn_bytes(x0 / s.astype(np.float64))
            out['vfs_scale'] = s
        else:
            out[k] = v
    return out


def reference(vfs_bytes, vfs_scale, p_lfs, n_lfs, W_hidden, b_hidden, W_embed, b_embed):
    return core(e4m3fn_values(vfs_bytes) * vfs_scale.astype(np.float64), p_lfs, n_lfs, W_hidden, b_hidden, W_embed, b_embed)

@@ -1,0 +1,467 @@
+from contextlib import ExitStack
+
+import concourse.mybir as mybir
+from concourse.masks import make_identity
+
+F32 = mybir.dt.float32
+BF16 = mybir.dt.bfloat16
+U32 = mybir.dt.uint32
+U8 = mybir.dt.uint8
+FP8 = mybir.dt.float8_e4m3fn
+FP8X4 = mybir.dt.float8_e4m3fn_x4
+ALU = mybir.AluOpType
+ACT = mybir.ActivationFunctionType
+AX = mybir.AxisListType
+
+P = 128
+B = 4096
+KV = 512
+KH = 512
+D = 128
+NNEG = 128
+ROWS = 4
+CW = ROWS * P
+NCH = 4
+
+FLOPS = 2 * B * KV * KH + 2 * B * KH * D
+
+SLOT = 57
+BN_J = list(range(6, 128, 10))
+
+
+def tile_hypernymvisual_acc_t_kernel(
+    tc, vfs_bytes, vfs_scale, p_lfs, n_lfs, W_hidden, b_hidden, W_embed, b_embed, out
+):
+    nc = tc.nc
+    with ExitStack() as ctx:
+        ctx.enter_context(tc.manual_schedule())
+        keep = ctx.enter_context(tc.tile_pool(name="keep", bufs=1))
+        pool = ctx.enter_context(tc.tile_pool(name="work", bufs=2))
+        psum = ctx.enter_context(tc.psum_pool(name="psum", bufs=1))
+
+        xb_view = vfs_bytes.rearrange("(p c q) k -> c p (q k)", c=8, q=ROWS)
+        out_view = out.rearrange("(p t) n -> p t n", t=32)
+
+        order = [0, 4, 5, 1, 6, 2, 7, 3]
+        raw = {}
+
+        def load_raw(c):
+            t = pool.tile([P, ROWS * KV], U8, name="raw", tag="raw", bufs=4)
+            nc.sync.dma_start(out=t[:], in_=xb_view[c])
+            raw[c] = t
+
+        wh = pool.tile([P, ROWS * KV], BF16, name="wide", tag="wide", bufs=2, align_bytes=64)
+        nc.sync.dma_start(out=wh[:].rearrange("p (t k) -> p t k", t=4), in_=W_hidden.rearrange("(m t) k -> m t k", t=4))
+        scale = keep.tile([P, KV], F32, name="scale")
+        nc.scalar.dma_start(out=scale[:], in_=vfs_scale.rearrange("o k -> (o k)").partition_broadcast(P))
+        load_raw(0)
+        load_raw(4)
+        we = keep.tile([P, KH], BF16, name="we", align_bytes=64)
+        nc.sync.dma_start(out=we[:], in_=W_embed)
+        nn = keep.tile([P, D], BF16, name="nn", align_bytes=64)
+        nc.sync.dma_start(out=nn[:], in_=n_lfs)
+        bh_raw = keep.tile([P, 4], BF16, name="bh_raw")
+        nc.scalar.dma_start(out=bh_raw[:], in_=b_hidden.rearrange("(m t) -> m t", t=4))
+        be_raw = keep.tile([P, 1], BF16, name="be_raw")
+        nc.scalar.dma_start(out=be_raw[:], in_=b_embed.rearrange("(d o) -> d o", o=1))
+        pp = keep.tile([P, 32 * D], BF16, name="pp")
+        nc.sync.dma_start(out=pp[:].rearrange("p (t d) -> p t d", t=32), in_=p_lfs.rearrange("(p t) d -> p t d", t=32))
+
+        one = keep.tile([P, 1], F32, name="one")
+        nc.vector.memset(one[:], 1.0)
+        one_out = keep.tile([P, 1], F32, name="one_out")
+        nc.scalar.activation(out=one_out[:], in_=one[:], func=ACT.Sqrt)
+        ident = keep.tile([P, P], F32, name="ident")
+        make_identity(nc, ident[:])
+        ident_b = keep.tile([P, P], BF16, name="ident_b")
+        nc.vector.tensor_copy(out=ident_b[:], in_=ident[:])
+
+        def bank(tag, bufs):
+            t = psum.tile([P, 512], F32, name=tag, tag=tag, bufs=bufs)
+            return t
+
+        def front_bank():
+            return bank("fr", 3)
+
+        def turn_pe(src, half):
+            words = src[:].bitcast(F32)
+            b = front_bank()
+            for q in (2 * half, 2 * half + 1):
+                for u in (0, 1):
+                    lo = 256 * (q % 2) + 128 * u
+                    nc.tensor.transpose(b[:, lo : lo + 128], words[:, 256 * q + u : 256 * (q + 1) : 2], ident[:])
+            return b
+
+        def turn_copy(b, grouped, half, eng):
+            dst = grouped[:].bitcast(F32)[:, 512 * half : 512 * (half + 1)].rearrange("p (q r u) -> p q r u", q=2, u=2)
+            srcv = b[:].rearrange("p (q u r) -> p q r u", q=2, u=2)
+            if eng == "v":
+                nc.vector.tensor_copy(out=dst, in_=srcv)
+            else:
+                nc.scalar.copy(out=dst, in_=srcv)
+
+        wg = pool.tile([P, 4 * CW], BF16, name="xg", tag="xg", bufs=2, align_bytes=64)
+        b0 = turn_pe(wh, 0)
+        b1 = turn_pe(wh, 1)
+        turn_copy(b0, wg, 0, "v")
+        turn_copy(b1, wg, 1, "s")
+        wc = keep.tile([P, CW], U32, name="wc", align_bytes=64)
+        ws = keep.tile([P, CW], U8, name="ws", align_bytes=64)
+        nc.vector.quantize_mx(out=wc[:].bitcast(FP8X4), scales=ws[:], in_=wg[:])
+
+        web = front_bank()
+        for u in (0, 1):
+            nc.tensor.transpose(web[:, 128 * u : 128 * (u + 1)], we[:].bitcast(F32)[:, u::2], ident[:])
+        weg = keep.tile([P, 4 * D], BF16, name="weg", align_bytes=64)
+        nc.scalar.copy(
+            out=weg[:].bitcast(F32).rearrange("p (r u) -> p r u", u=2),
+            in_=web[:, 0:256].rearrange("p (u r) -> p r u", u=2),
+        )
+        wec = keep.tile([P, D], U32, name="wec", align_bytes=64)
+        wes = keep.tile([P, D], U8, name="wes", align_bytes=64)
+        nc.vector.quantize_mx(out=wec[:].bitcast(FP8X4), scales=wes[:], in_=weg[:])
+
+        nb = psum.tile([P, D], BF16, name="fr", tag="fr", bufs=3)
+        nc.tensor.transpose(nb[:], nn[:], ident_b[:])
+        nT = keep.tile([P, NNEG], BF16, name="nT")
+        nc.vector.tensor_copy(out=nT[:], in_=nb[:])
+        nTf = keep.tile([P, NNEG], F32, name="nTf")
+        nc.vector.tensor_copy(out=nTf[:], in_=nT[:])
+        bh = keep.tile([P, 1, 4], F32, name="bh")
+        nc.vector.tensor_copy(out=bh[:, 0, :], in_=bh_raw[:])
+        be = keep.tile([P, 1], F32, name="be")
+        nc.vector.tensor_copy(out=be[:], in_=be_raw[:])
+
+        eT = {}
+        eB = {}
+        GL = {}
+        ST = {}
+        ESQ = {}
+
+        def front(c):
+            st = {}
+            mask = c >= NCH
+
+            def widen(q):
+                if q == 0:
+                    st["w"] = pool.tile([P, ROWS * KV], BF16, name="wide", tag="wide", bufs=2, align_bytes=64)
+                    st["xg"] = pool.tile([P, 4 * CW], BF16, name="xg", tag="xg", bufs=2, align_bytes=64)
+                k = slice(KV * q, KV * (q + 1))
+                nc.vector.tensor_tensor(out=st["w"][:, k], in0=raw[c][:, k].bitcast(FP8), in1=scale[:], op=ALU.mult)
+
+            def turn(half):
+                st["b%d" % half] = turn_pe(st["w"], half)
+
+            def copy(half):
+                turn_copy(st["b%d" % half], st["xg"], half, "s")
+
+            def quant_x():
+                st["xc"] = pool.tile([P, CW], U32, name="xc", tag="xc", bufs=2, align_bytes=64)
+                st["xs"] = pool.tile([P, CW], U8, name="xs", tag="xs", bufs=2, align_bytes=64)
+                nc.vector.quantize_mx(out=st["xc"][:].bitcast(FP8X4), scales=st["xs"][:], in_=st["xg"][:])
+
+            def stage1(q):
+                b = front_bank()
+                r = slice(P * q, P * (q + 1))
+                for t in range(4):
+                    m = slice(P * t, P * (t + 1))
+                    nc.tensor.matmul_mx(
+                        out=b[:, m], lhsT=wc[:, m].bitcast(FP8X4), lhsT_scale=ws[:, m],
+                        rhs=st["xc"][:, r].bitcast(FP8X4), rhs_scale=st["xs"][:, r], start=True, stop=True,
+                    )
+                st["h%d" % q] = b
+
+            def hidden(q):
+                if q == 0:
+                    st["hg"] = pool.tile([P, 4 * CW], BF16, name="hg", tag="hg", bufs=2, align_bytes=64)
+                nc.vector.tensor_tensor(
+                    out=st["hg"][:, 512 * q : 512 * (q + 1)].rearrange("p (r t) -> p r t", t=4),
+                    in0=st["h%d" % q][:].rearrange("p (t r) -> p r t", t=4),
+                    in1=bh[:].to_broadcast([P, P, 4]),
+                    op=ALU.add,
+                )
+
+            def quant_h():
+                st["hc"] = pool.tile([P, CW], U32, name="hc", tag="hc", bufs=2, align_bytes=64)
+                st["hs"] = pool.tile([P, CW], U8, name="hs", tag="hs", bufs=2, align_bytes=64)
+                nc.vector.quantize_mx(out=st["hc"][:].bitcast(FP8X4), scales=st["hs"][:], in_=st["hg"][:])
+
+            def stage2():
+                b = front_bank()
+                nc.tensor.matmul_mx(
+                    out=b[:], lhsT=wec[:].bitcast(FP8X4), lhsT_scale=wes[:],
+                    rhs=st["hc"][:].bitcast(FP8X4), rhs_scale=st["hs"][:], start=True, stop=True,
+                )
+                st["e"] = b
+
+            def ecopy():
+                t = pool.tile([P, CW], F32, name="eT", tag="eT", bufs=4)
+                nc.scalar.activation(out=t[:], in_=st["e"][:], func=ACT.Identity, bias=be[:])
+                eT[c] = t
+
+            def split_a():
+                if mask:
+                    t = pool.tile([P, CW], BF16, name="eB", tag="eB", bufs=2)
+                    nc.vector.tensor_copy(out=t[:], in_=eT[c][:])
+                    eB[c] = t
+
+            def split_b():
+                if mask:
+                    g = pool.tile([P, 2, CW], BF16, name="GL", tag="GL", bufs=2)
+                    d = pool.tile([P, CW], BF16, name="dl", tag="dl", bufs=2)
+                    nc.vector.scalar_tensor_tensor(
+                        out=d[:], in0=eT[c][:], scalar=-1.0, in1=eB[c][:], op0=ALU.mult, op1=ALU.add
+                    )
+                    nc.vector.tensor_scalar(out=g[:, 0, :], in0=eB[c][:], scalar1=-1.0, scalar2=None, op0=ALU.mult)
+                    nc.vector.tensor_scalar(out=g[:, 1, :], in0=d[:], scalar1=2.0, scalar2=None, op0=ALU.mult)
+                    GL[c] = g
+
+            def eback():
+                b = front_bank()
+                for q in range(ROWS):
+                    r = slice(P * q, P * (q + 1))
+                    nc.tensor.transpose(b[:, r], eT[c][:, r], ident[:])
+                st["eb"] = b
+
+            def pdiff():
+                t = pool.tile([P, CW], F32, name="xp", tag="xp", bufs=2)
+                nc.vector.tensor_tensor(out=t[:], in0=pp[:, CW * c : CW * (c + 1)], in1=st["eb"][:], op=ALU.subtract)
+                st["xp"] = t
+                s = pool.tile([P, ROWS, NNEG + 1], F32, name="ST", tag="ST", bufs=4)
+                ST[c] = s
+                if mask:
+                    q2 = pool.tile([P, ROWS], F32, name="esq", tag="esq", bufs=2)
+                    ESQ[c] = q2
+                    for q in range(ROWS):
+                        junk = pool.tile([P, P], BF16, name="junk", tag="junk", bufs=8)
+                        nc.scalar.activation(
+                            out=junk[:], in_=st["eb"][:, P * q : P * (q + 1)], func=ACT.Square, accum_out=q2[:, q : q + 1]
+                        )
+
+            def psum2(q):
+                j2 = pool.tile([P, P], F32, name="junkp", tag="junkp", bufs=2)
+                x = st["xp"][:, P * q : P * (q + 1)]
+                nc.vector.scalar_tensor_tensor(
+                    out=j2[:], in0=x, scalar=0.0, in1=x, op0=ALU.max, op1=ALU.mult, accum_out=ST[c][:, q, 0:1]
+                )
+
+            return [
+                [lambda: widen(0)],
+                [lambda: widen(1)],
+                [lambda: turn(0), lambda: widen(2)],
+                [lambda: copy(0), lambda: widen(3)],
+                [lambda: turn(1)],
+                [lambda: copy(1)],
+                [quant_x],
+                [lambda: stage1(0)],
+                [lambda: hidden(0), lambda: stage1(1)],
+                [lambda: hidden(1), lambda: stage1(2)],
+                [lambda: hidden(2), lambda: stage1(3)],
+                [lambda: hidden(3)],
+                [quant_h],
+                [stage2],
+                [ecopy],
+                [split_a, eback],
+                [pdiff],
+                [split_b],
+                [lambda: psum2(0), lambda: psum2(1)],
+                [lambda: psum2(2), lambda: psum2(3)],
+            ]
+
+        def run(piece):
+            for fn in piece:
+                fn()
+
+        fa = front(0)
+        fm = front(4)
+        for i in range(len(fa)):
+            run(fa[i])
+            run(fm[i])
+        for c in order[2:]:
+            load_raw(c)
+
+        pieces = {}
+        for c, start in ((5, 2), (1, 60), (6, 126), (2, 180), (7, 250), (3, 310)):
+            for i, piece in enumerate(front(c)):
+                pieces[start + 2 * i] = piece
+
+        due = {}
+
+        def later(s, fn):
+            due.setdefault(s, []).append(fn)
+
+        MT = {}
+        queue = []
+
+        def make_planes(k, o):
+            c = NCH + k // 2
+            h = k % 2
+            if o == 0:
+                MT[k] = pool.tile([P, NNEG, 256], BF16, name="MT", tag="MT", bufs=2)
+            for j in range(128 * o // SLOT, 128 * (o + 1) // SLOT):
+                nc.vector.tensor_scalar(
+                    out=MT[k][:, j, :], in0=eB[c][:, 256 * h : 256 * (h + 1)],
+                    scalar1=nTf[:, j : j + 1], scalar2=None, op0=ALU.max,
+                )
+
+        def mask_ops(k):
+            c = NCH + k // 2
+            h = k % 2
+            ops = []
+            for u in (0, 1):
+                q = 2 * h + u
+                cell = {}
+
+                def uop(i, u=u, q=q, cell=cell):
+                    if i == 0:
+                        cell["U"] = bank("U", 1)
+                    nc.tensor.matmul(
+                        cell["U"][:, 2 * i : 2 * i + 2], lhsT=MT[k][:, :, P * u + i],
+                        rhs=GL[c][:, :, P * q + i], start=True, stop=True,
+                    )
+
+                def t3(q=q, cell=cell):
+                    cell["R"] = bank("R", 1)
+                    nc.tensor.matmul(
+                        cell["R"][:, 0:P], lhsT=GL[c][:, 0, P * q : P * (q + 1)], rhs=nT[:], start=True, stop=False
+                    )
+
+                def rop(j, u=u, cell=cell):
+                    nc.tensor.matmul(
+                        cell["R"][:, j : j + 1], lhsT=MT[k][:, j, P * u : P * (u + 1)],
+                        rhs=nT[:, j : j + 1], start=False, stop=(j == NNEG - 1),
+                    )
+
+                def reduce_u(cell=cell):
+                    us = pool.tile([P, P], F32, name="us", tag="us", bufs=2)
+                    nc.vector.tensor_reduce(
+                        out=us[:], in_=cell["U"][:, 0:256].rearrange("p (i a) -> p i a", a=2), axis=AX.X, op=ALU.add
+                    )
+                    cell["us"] = us
+
+                def turn_u(cell=cell):
+                    b = front_bank()
+                    nc.tensor.transpose(b[:, 0:P], cell["us"][:], ident[:])
+                    cell["ut"] = b
+
+                def add_u(q=q, cell=cell):
+                    t1 = pool.tile([P, P], F32, name="t1", tag="t1", bufs=2)
+                    nc.vector.tensor_scalar(
+                        out=t1[:], in0=cell["ut"][:, 0:P], scalar1=ESQ[c][:, q : q + 1], scalar2=None, op0=ALU.add
+                    )
+                    cell["t1"] = t1
+
+                def add_r(q=q, cell=cell):
+                    nc.vector.tensor_tensor(
+                        out=ST[c][:, q, 1 : NNEG + 1], in0=cell["R"][:, 0:P], in1=cell["t1"][:], op=ALU.add
+                    )
+
+                def store():
+                    v = ST[c][:, 2 * h : 2 * h + 2, :]
+                    o = pool.tile([P, 2, NNEG + 1], F32, name="om", tag="om", bufs=2)
+                    nc.vector.tensor_scalar(out=v, in0=v, scalar1=0.0, scalar2=None, op0=ALU.max)
+                    nc.scalar.activation(out=o[:], in_=v, func=ACT.Sqrt)
+                    return o
+
+                for i in range(P):
+                    ops.append((lambda i=i, uop=uop: uop(i), [(1, reduce_u), (3, turn_u), (5, add_u)] if i == P - 1 else []))
+                ops.append((t3, []))
+                tail = [(1, add_r)]
+                if u == 1:
+                    cell2 = {}
+
+                    def root(cell2=cell2, store=store):
+                        cell2["o"] = store()
+
+                    def neg(cell2=cell2):
+                        o = cell2["o"]
+                        nc.vector.tensor_scalar(out=o[:], in0=o[:], scalar1=-1.0, scalar2=None, op0=ALU.mult)
+                        t0 = 4 * c + 2 * h
+                        nc.sync.dma_start(out=out_view[:, t0 : t0 + 2, :], in_=o[:])
+
+                    tail = tail + [(2, root), (4, neg)]
+                for j in range(NNEG):
+                    ops.append((lambda j=j, rop=rop: rop(j), tail if j == NNEG - 1 else []))
+            return ops
+
+        BN = {}
+
+        def bn_bank(b, a, n):
+            for h in (0, 1):
+                nc.vector.bn_stats(
+                    out=BN[a][:, 2 * n + h, :], in_=b[:, 256 * h : 256 * (h + 1)].rearrange("p (b d) -> p d b", b=2)
+                )
+
+        def bn_post(a):
+            n = len(BN_J)
+            v = BN[a][:].rearrange("p g (b e) -> p (g b) e", e=3)
+            m2 = pool.tile([P, 4 * n], F32, name="m2", tag="m2", bufs=2)
+            nc.vector.tensor_tensor(out=m2[:], in0=v[:, :, 1], in1=v[:, :, 1], op=ALU.mult)
+            dst = ST[a][:, :, 1 + BN_J[0] : 2 + BN_J[-1] : BN_J[1] - BN_J[0]].rearrange("p q n -> p n q")
+            nc.vector.scalar_tensor_tensor(
+                out=dst, in0=m2[:].rearrange("p (n q) -> p n q", q=4), scalar=128.0,
+                in1=v[:, :, 2].rearrange("p (n q) -> p n q", q=4), op0=ALU.mult, op1=ALU.add,
+            )
+
+        OUTA = {}
+
+        def a_sqrt(a):
+            o = pool.tile([P, ROWS, NNEG + 1], F32, name="oa", tag="oa", bufs=2)
+            nc.scalar.activation(out=o[:], in_=ST[a][:], func=ACT.Sqrt)
+            OUTA[a] = o
+
+        def a_store(a):
+            o = OUTA[a]
+            nc.vector.tensor_scalar(out=o[:], in0=o[:], scalar1=-1.0, scalar2=None, op0=ALU.mult)
+            nc.sync.dma_start(out=out_view[:, ROWS * a : ROWS * (a + 1), :], in_=o[:])
+
+        def direct(s):
+            a = s // 128
+            j = s % 128
+            if j == 0:
+                BN[a] = pool.tile([P, 2 * len(BN_J), 6], F32, name="BN", tag="BN", bufs=2)
+            r = pool.tile([P, CW], F32, name="r", tag="r", bufs=4)
+            nc.vector.tensor_scalar(
+                out=r[:], in0=eT[a][:], scalar1=nTf[:, j : j + 1], scalar2=0.0, op0=ALU.subtract, op1=ALU.min
+            )
+            b = bank("tr", 3)
+            for q in range(ROWS):
+                nc.tensor.transpose(b[:, P * q : P * (q + 1)], r[:, P * q : P * (q + 1)], ident[:])
+            if j in BN_J:
+                later(s + 2, lambda b=b, a=a, n=BN_J.index(j): bn_bank(b, a, n))
+            else:
+                for q in range(ROWS):
+                    junk = pool.tile([P, P], BF16, name="junk", tag="junk", bufs=8)
+                    nc.scalar.activation(
+                        out=junk[:], in_=b[:, P * q : P * (q + 1)], func=ACT.Square, accum_out=ST[a][:, q, 1 + j : 2 + j]
+                    )
+            if j == 127:
+                later(s + 4, lambda a=a: bn_post(a))
+                later(s + 6, lambda a=a: a_sqrt(a))
+                later(s + 8, lambda a=a: a_store(a))
+
+        total = 512
+        head = 0
+        for s in range(total + 20):
+            for fn in due.get(s, []):
+                fn()
+            if s in pieces:
+                run(pieces[s])
+            if s < total:
+                direct(s)
+            k = s // SLOT
+            o = s % SLOT
+            if k < 8:
+                make_planes(k, o)
+            if o == 0 and 1 <= k <= 8:
+                queue.extend(mask_ops(k - 1))
+            left = SLOT - o
+            if k > 8 or s >= total - 1:
+                left = 1
+            n = (len(queue) - head + left - 1) // left
+            for i in range(n):
+                fn, events = queue[head]
+                head += 1
+                fn()
+                for d, ev in events:
+                    later(s + d, ev)

@@ -24,9 +24,8 @@ CW = ROWS * P
 NCH = 4
 
 FLOPS = 2 * B * KV * KH + 2 * B * KH * D
-
-SLOT = 57
-BN_J = list(range(6, 128, 10))
+WARM = True
+FR = 3
 
 
 def tile_hypernymvisual_acc_t_kernel(
@@ -42,7 +41,7 @@ def tile_hypernymvisual_acc_t_kernel(
         xb_view = vfs_bytes.rearrange("(p c q) k -> c p (q k)", c=8, q=ROWS)
         out_view = out.rearrange("(p t) n -> p t n", t=32)
 
-        order = [0, 4, 5, 1, 6, 2, 7, 3]
+        order = [0, 4, 1, 5, 2, 6, 3, 7]
         raw = {}
 
         def load_raw(c):
@@ -50,6 +49,8 @@ def tile_hypernymvisual_acc_t_kernel(
             nc.sync.dma_start(out=t[:], in_=xb_view[c])
             raw[c] = t
 
+        nn = keep.tile([P, D], BF16, name="nn", align_bytes=64)
+        nc.sync.dma_start(out=nn[:], in_=n_lfs)
         wh = pool.tile([P, ROWS * KV], BF16, name="wide", tag="wide", bufs=2, align_bytes=64)
         nc.sync.dma_start(out=wh[:].rearrange("p (t k) -> p t k", t=4), in_=W_hidden.rearrange("(m t) k -> m t k", t=4))
         scale = keep.tile([P, KV], F32, name="scale")
@@ -58,12 +59,12 @@ def tile_hypernymvisual_acc_t_kernel(
         load_raw(4)
         we = keep.tile([P, KH], BF16, name="we", align_bytes=64)
         nc.sync.dma_start(out=we[:], in_=W_embed)
-        nn = keep.tile([P, D], BF16, name="nn", align_bytes=64)
-        nc.sync.dma_start(out=nn[:], in_=n_lfs)
         bh_raw = keep.tile([P, 4], BF16, name="bh_raw")
         nc.scalar.dma_start(out=bh_raw[:], in_=b_hidden.rearrange("(m t) -> m t", t=4))
         be_raw = keep.tile([P, 1], BF16, name="be_raw")
         nc.scalar.dma_start(out=be_raw[:], in_=b_embed.rearrange("(d o) -> d o", o=1))
+        bew_raw = keep.tile([P, D], BF16, name="bew_raw")
+        nc.scalar.dma_start(out=bew_raw[:], in_=b_embed.partition_broadcast(P))
         pp = keep.tile([P, 32 * D], BF16, name="pp")
         nc.sync.dma_start(out=pp[:].rearrange("p (t d) -> p t d", t=32), in_=p_lfs.rearrange("(p t) d -> p t d", t=32))
 
@@ -81,7 +82,7 @@ def tile_hypernymvisual_acc_t_kernel(
             return t
 
         def front_bank():
-            return bank("fr", 3)
+            return bank("fr", FR)
 
         def turn_pe(src, half):
             words = src[:].bitcast(F32)
@@ -121,7 +122,7 @@ def tile_hypernymvisual_acc_t_kernel(
         wes = keep.tile([P, D], U8, name="wes", align_bytes=64)
         nc.vector.quantize_mx(out=wec[:].bitcast(FP8X4), scales=wes[:], in_=weg[:])
 
-        nb = psum.tile([P, D], BF16, name="fr", tag="fr", bufs=3)
+        nb = psum.tile([P, D], BF16, name="fr", tag="fr", bufs=FR)
         nc.tensor.transpose(nb[:], nn[:], ident_b[:])
         nT = keep.tile([P, NNEG], BF16, name="nT")
         nc.vector.tensor_copy(out=nT[:], in_=nb[:])
@@ -131,16 +132,31 @@ def tile_hypernymvisual_acc_t_kernel(
         nc.vector.tensor_copy(out=bh[:, 0, :], in_=bh_raw[:])
         be = keep.tile([P, 1], F32, name="be")
         nc.vector.tensor_copy(out=be[:], in_=be_raw[:])
+        bew = keep.tile([P, 1, D], F32, name="bew")
+        nc.vector.tensor_copy(out=bew[:, 0, :], in_=bew_raw[:])
 
+        NB = keep.tile([P, D, NNEG], BF16, name="NB")
+
+        def spread(x):
+            b = psum.tile([P, 8, P], BF16, name="fr", tag="fr", bufs=FR)
+            for i in range(8):
+                d = 8 * x + i
+                nc.tensor.transpose(b[:, i, :], nn[:, d : d + 1].to_broadcast([P, P]), ident_b[:])
+            if x % 2:
+                nc.vector.tensor_copy(out=NB[:, 8 * x : 8 * x + 8, :], in_=b[:])
+            else:
+                nc.scalar.copy(out=NB[:, 8 * x : 8 * x + 8, :], in_=b[:])
+
+        E = {}
         eT = {}
         eB = {}
         GL = {}
         ST = {}
-        ESQ = {}
+        ROWC = {}
 
         def front(c):
             st = {}
-            mask = c >= NCH
+            thin = c >= NCH
 
             def widen(q):
                 if q == 0:
@@ -188,25 +204,47 @@ def tile_hypernymvisual_acc_t_kernel(
 
             def stage2():
                 b = front_bank()
-                nc.tensor.matmul_mx(
-                    out=b[:], lhsT=wec[:].bitcast(FP8X4), lhsT_scale=wes[:],
-                    rhs=st["hc"][:].bitcast(FP8X4), rhs_scale=st["hs"][:], start=True, stop=True,
-                )
+                if thin:
+                    nc.tensor.matmul_mx(
+                        out=b[:], lhsT=wec[:].bitcast(FP8X4), lhsT_scale=wes[:],
+                        rhs=st["hc"][:].bitcast(FP8X4), rhs_scale=st["hs"][:], start=True, stop=True,
+                    )
+                else:
+                    for q in range(ROWS):
+                        r = slice(P * q, P * (q + 1))
+                        nc.tensor.matmul_mx(
+                            out=b[:, r], lhsT=st["hc"][:, r].bitcast(FP8X4), lhsT_scale=st["hs"][:, r],
+                            rhs=wec[:].bitcast(FP8X4), rhs_scale=wes[:], start=True, stop=True,
+                        )
                 st["e"] = b
 
             def ecopy():
-                t = pool.tile([P, CW], F32, name="eT", tag="eT", bufs=4)
-                nc.scalar.activation(out=t[:], in_=st["e"][:], func=ACT.Identity, bias=be[:])
-                eT[c] = t
+                if thin:
+                    t = pool.tile([P, CW], F32, name="eT", tag="eT", bufs=2)
+                    nc.scalar.activation(out=t[:], in_=st["e"][:], func=ACT.Identity, bias=be[:])
+                    eT[c] = t
+                else:
+                    t = pool.tile([P, CW], F32, name="E", tag="E", bufs=2)
+                    nc.vector.tensor_tensor(
+                        out=t[:].rearrange("p (q d) -> p q d", d=D), in0=st["e"][:].rearrange("p (q d) -> p q d", d=D),
+                        in1=bew[:].to_broadcast([P, ROWS, D]), op=ALU.add,
+                    )
+                    E[c] = t
+                    st["eb"] = t
 
-            def split_a():
-                if mask:
+            def eback():
+                if thin:
                     t = pool.tile([P, CW], BF16, name="eB", tag="eB", bufs=2)
                     nc.vector.tensor_copy(out=t[:], in_=eT[c][:])
                     eB[c] = t
+                    b = front_bank()
+                    for q in range(ROWS):
+                        r = slice(P * q, P * (q + 1))
+                        nc.tensor.transpose(b[:, r], eT[c][:, r], ident[:])
+                    st["eb"] = b
 
             def split_b():
-                if mask:
+                if thin:
                     g = pool.tile([P, 2, CW], BF16, name="GL", tag="GL", bufs=2)
                     d = pool.tile([P, CW], BF16, name="dl", tag="dl", bufs=2)
                     nc.vector.scalar_tensor_tensor(
@@ -216,27 +254,41 @@ def tile_hypernymvisual_acc_t_kernel(
                     nc.vector.tensor_scalar(out=g[:, 1, :], in0=d[:], scalar1=2.0, scalar2=None, op0=ALU.mult)
                     GL[c] = g
 
-            def eback():
-                b = front_bank()
-                for q in range(ROWS):
-                    r = slice(P * q, P * (q + 1))
-                    nc.tensor.transpose(b[:, r], eT[c][:, r], ident[:])
-                st["eb"] = b
-
-            def pdiff():
+            def rows_a():
+                h = pool.tile([P, CW], BF16, name="er", tag="er", bufs=2)
+                nc.vector.tensor_copy(out=h[:], in_=st["eb"][:])
                 t = pool.tile([P, CW], F32, name="xp", tag="xp", bufs=2)
                 nc.vector.tensor_tensor(out=t[:], in0=pp[:, CW * c : CW * (c + 1)], in1=st["eb"][:], op=ALU.subtract)
                 st["xp"] = t
                 s = pool.tile([P, ROWS, NNEG + 1], F32, name="ST", tag="ST", bufs=4)
                 ST[c] = s
-                if mask:
-                    q2 = pool.tile([P, ROWS], F32, name="esq", tag="esq", bufs=2)
-                    ESQ[c] = q2
+                d = pool.tile([P, CW], F32, name="ed", tag="ed", bufs=2)
+                nc.vector.tensor_tensor(out=d[:], in0=h[:], in1=st["eb"][:], op=ALU.subtract)
+                st["ed"] = d
+
+            def rows_b():
+                q2 = pool.tile([P, 2, ROWS], F32, name="q2", tag="q2", bufs=2)
+                for q in range(ROWS):
+                    junk = pool.tile([P, P], BF16, name="junk", tag="junk", bufs=4)
+                    nc.scalar.activation(
+                        out=junk[:], in_=st["ed"][:, P * q : P * (q + 1)], func=ACT.Square, accum_out=q2[:, 0, q : q + 1]
+                    )
+                if thin:
                     for q in range(ROWS):
-                        junk = pool.tile([P, P], BF16, name="junk", tag="junk", bufs=8)
+                        junk = pool.tile([P, P], BF16, name="junk", tag="junk", bufs=4)
                         nc.scalar.activation(
-                            out=junk[:], in_=st["eb"][:, P * q : P * (q + 1)], func=ACT.Square, accum_out=q2[:, q : q + 1]
+                            out=junk[:], in_=st["eb"][:, P * q : P * (q + 1)], func=ACT.Square, accum_out=q2[:, 1, q : q + 1]
                         )
+                st["q2"] = q2
+
+            def rows_c():
+                q2 = st["q2"]
+                r = pool.tile([P, ROWS], F32, name="rowc", tag="rowc", bufs=4)
+                if thin:
+                    nc.vector.tensor_tensor(out=r[:], in0=q2[:, 1, :], in1=q2[:, 0, :], op=ALU.subtract)
+                else:
+                    nc.vector.tensor_scalar(out=r[:], in0=q2[:, 0, :], scalar1=-1.0, scalar2=None, op0=ALU.mult)
+                ROWC[c] = r
 
             def psum2(q):
                 j2 = pool.tile([P, P], F32, name="junkp", tag="junkp", bufs=2)
@@ -261,10 +313,10 @@ def tile_hypernymvisual_acc_t_kernel(
                 [quant_h],
                 [stage2],
                 [ecopy],
-                [split_a, eback],
-                [pdiff],
-                [split_b],
-                [lambda: psum2(0), lambda: psum2(1)],
+                [eback],
+                [rows_a],
+                [rows_b, split_b],
+                [rows_c, lambda: psum2(0), lambda: psum2(1)],
                 [lambda: psum2(2), lambda: psum2(3)],
             ]
 
@@ -272,196 +324,219 @@ def tile_hypernymvisual_acc_t_kernel(
             for fn in piece:
                 fn()
 
-        fa = front(0)
+        fd = front(0)
         fm = front(4)
-        for i in range(len(fa)):
-            run(fa[i])
+        for i in range(len(fd)):
+            run(fd[i])
+            if i < 16:
+                spread(i)
             run(fm[i])
         for c in order[2:]:
             load_raw(c)
 
         pieces = {}
-        for c, start in ((5, 2), (1, 60), (6, 126), (2, 180), (7, 250), (3, 310)):
-            for i, piece in enumerate(front(c)):
-                pieces[start + 2 * i] = piece
+        for x in range(1, 4):
+            for c, start in ((x, 64 * x - 62), (x + 4, 64 * x - 61)):
+                for i, piece in enumerate(front(c)):
+                    pieces.setdefault(start + 2 * i, []).extend(piece)
 
         due = {}
 
         def later(s, fn):
             due.setdefault(s, []).append(fn)
 
-        MT = {}
-        queue = []
+        NG = 256
+        MD = {}
+        SD = {}
+        MI = {}
+        MJ = {}
+        ACC = {}
+        UB = {}
+        RBANK = bank("R", 1)
 
-        def make_planes(k, o):
-            c = NCH + k // 2
-            h = k % 2
-            if o == 0:
-                MT[k] = pool.tile([P, NNEG, 256], BF16, name="MT", tag="MT", bufs=2)
-            for j in range(128 * o // SLOT, 128 * (o + 1) // SLOT):
+        def planes(g):
+            tile = g // 16
+            c = tile // 4
+            d0 = 8 * (g % 16)
+            k = g // 32
+            cm = NCH + k // 2
+            i0 = 256 * (k % 2) + 8 * (g % 32)
+            j0 = 4 * (g % 32)
+            md = pool.tile([P, 8, NNEG], BF16, name="md", tag="md", bufs=3)
+            sd = pool.tile([P, 8, NNEG], F32, name="sd", tag="sd", bufs=3)
+            mi = pool.tile([P, 8, NNEG], BF16, name="mi", tag="mi", bufs=3)
+            mj = pool.tile([P, 4, 256], BF16, name="mj", tag="mj", bufs=3)
+            MD[g] = md
+            SD[g] = sd
+            MI[g] = mi
+            MJ[g] = mj
+            for x in range(8):
+                col = D * (tile % 4) + d0 + x
                 nc.vector.tensor_scalar(
-                    out=MT[k][:, j, :], in0=eB[c][:, 256 * h : 256 * (h + 1)],
-                    scalar1=nTf[:, j : j + 1], scalar2=None, op0=ALU.max,
+                    out=md[:, x, :], in0=NB[:, d0 + x, :], scalar1=E[c][:, col : col + 1], scalar2=None, op0=ALU.max
+                )
+                nc.scalar.activation(
+                    out=sd[:, x, :], in_=md[:, x, :], func=ACT.Square, bias=E[c][:, col : col + 1], scale=-1.0
+                )
+            for x in range(8):
+                nc.vector.tensor_scalar(
+                    out=mi[:, x, :], in0=nT[:], scalar1=eT[cm][:, i0 + x : i0 + x + 1], scalar2=None, op0=ALU.max
+                )
+            h = 256 * (k % 2)
+            for x in range(4):
+                nc.vector.tensor_scalar(
+                    out=mj[:, x, :], in0=eB[cm][:, h : h + 256], scalar1=nTf[:, j0 + x : j0 + x + 1], scalar2=None, op0=ALU.max
                 )
 
-        def mask_ops(k):
-            c = NCH + k // 2
+        def adds(g, s):
+            tile = g // 16
+            if g % 16 == 0:
+                ACC[tile] = bank("acc", 2)
+            for x in range(8):
+                nc.tensor.matmul(
+                    ACC[tile][:, 0:P], lhsT=SD[g][:, x, :], rhs=ident[:], is_transpose=True,
+                    start=(g % 16 == 0 and x == 0), stop=(g % 16 == 15 and x == 7),
+                )
+            if g % 16 == 15:
+                finish_direct(tile, s)
+
+        def finish_direct(tile, s):
+            c = tile // 4
+            q = tile % 4
+            cell = {}
+
+            def f0():
+                t = pool.tile([P, P], F32, name="us", tag="us", bufs=3)
+                nc.scalar.copy(out=t[:], in_=ACC[tile][:, 0:P])
+                cell["t"] = t
+
+            def f1():
+                b = front_bank()
+                nc.tensor.transpose(b[:, 0:P], cell["t"][:], ident[:])
+                cell["b"] = b
+
+            def f2():
+                nc.vector.tensor_scalar(
+                    out=ST[c][:, q, 1 : NNEG + 1], in0=cell["b"][:, 0:P], scalar1=ROWC[c][:, q : q + 1], scalar2=0.0,
+                    op0=ALU.add, op1=ALU.max,
+                )
+
+            later(s + 1, f0)
+            later(s + 2, f1)
+            later(s + 3, f2)
+            if q % 2:
+                store(c, q // 2, s + 4)
+
+        def store(c, h, s):
+            cell = {}
+
+            def f0():
+                o = pool.tile([P, 2, NNEG + 1], F32, name="om", tag="om", bufs=3)
+                nc.scalar.activation(out=o[:], in_=ST[c][:, 2 * h : 2 * h + 2, :], func=ACT.Sqrt)
+                cell["o"] = o
+
+            def f1():
+                o = cell["o"]
+                nc.vector.tensor_scalar(out=o[:], in0=o[:], scalar1=-1.0, scalar2=None, op0=ALU.mult)
+                t0 = ROWS * c + 2 * h
+                nc.sync.dma_start(out=out_view[:, t0 : t0 + 2, :], in_=o[:])
+
+            later(s, f0)
+            later(s + 1, f1)
+
+        def thins(g, s):
+            k = g // 32
+            cm = NCH + k // 2
+            u = (g % 32) // 16
+            q = 2 * (k % 2) + u
+            if g % 16 == 0:
+                UB[g // 16] = bank("U", 2)
+            ub = UB[g // 16]
+            for x in range(8):
+                i = 8 * (g % 16) + x
+                nc.tensor.matmul(
+                    ub[:, 2 * i : 2 * i + 2], lhsT=MI[g][:, x, :], rhs=GL[cm][:, :, P * q + i], start=True, stop=True
+                )
+            if g % 16 == 15:
+                nc.tensor.matmul(
+                    ub[:, 256:384], lhsT=nT[:], rhs=GL[cm][:, 0, P * q : P * (q + 1)], start=True, stop=True
+                )
+                finish_u(k, u, g // 16, s)
+            rb = RBANK[:, 256 * (k % 2) : 256 * (k % 2 + 1)]
+            for x in range(4):
+                j = 4 * (g % 32) + x
+                for v in (0, 1):
+                    nc.tensor.matmul(
+                        rb[:, P * v + j : P * v + j + 1], lhsT=MJ[g][:, x, P * v : P * (v + 1)], rhs=nT[:, j : j + 1],
+                        start=True, stop=True,
+                    )
+            if g % 32 == 31:
+                finish_r(k, s)
+
+        UT = {}
+
+        def finish_u(k, u, key, s):
+            cm = NCH + k // 2
+            q = 2 * (k % 2) + u
+            cell = {}
+
+            def f0():
+                t = pool.tile([P, P], F32, name="u0", tag="u0", bufs=2)
+                nc.vector.tensor_reduce(
+                    out=t[:], in_=UB[key][:, 0:256].rearrange("p (i a) -> p i a", a=2), axis=AX.X, op=ALU.add
+                )
+                t2 = pool.tile([P, P], F32, name="us", tag="us", bufs=3)
+                nc.vector.tensor_tensor(out=t2[:], in0=UB[key][:, 256:384], in1=t[:], op=ALU.add)
+                cell["t"] = t2
+
+            def f1():
+                b = front_bank()
+                nc.tensor.transpose(b[:, 0:P], cell["t"][:], ident[:])
+                cell["b"] = b
+
+            def f2():
+                t1 = pool.tile([P, P], F32, name="t1", tag="t1", bufs=4)
+                nc.vector.tensor_scalar(
+                    out=t1[:], in0=cell["b"][:, 0:P], scalar1=ROWC[cm][:, q : q + 1], scalar2=None, op0=ALU.add
+                )
+                UT[2 * k + u] = t1
+
+            later(s + 1, f0)
+            later(s + 2, f1)
+            later(s + 3, f2)
+
+        def finish_r(k, s):
+            cm = NCH + k // 2
             h = k % 2
-            ops = []
-            for u in (0, 1):
-                q = 2 * h + u
-                cell = {}
 
-                def uop(i, u=u, q=q, cell=cell):
-                    if i == 0:
-                        cell["U"] = bank("U", 1)
-                    nc.tensor.matmul(
-                        cell["U"][:, 2 * i : 2 * i + 2], lhsT=MT[k][:, :, P * u + i],
-                        rhs=GL[c][:, :, P * q + i], start=True, stop=True,
-                    )
-
-                def t3(q=q, cell=cell):
-                    cell["R"] = bank("R", 1)
-                    nc.tensor.matmul(
-                        cell["R"][:, 0:P], lhsT=GL[c][:, 0, P * q : P * (q + 1)], rhs=nT[:], start=True, stop=False
-                    )
-
-                def rop(j, u=u, cell=cell):
-                    nc.tensor.matmul(
-                        cell["R"][:, j : j + 1], lhsT=MT[k][:, j, P * u : P * (u + 1)],
-                        rhs=nT[:, j : j + 1], start=False, stop=(j == NNEG - 1),
-                    )
-
-                def reduce_u(cell=cell):
-                    us = pool.tile([P, P], F32, name="us", tag="us", bufs=2)
-                    nc.vector.tensor_reduce(
-                        out=us[:], in_=cell["U"][:, 0:256].rearrange("p (i a) -> p i a", a=2), axis=AX.X, op=ALU.add
-                    )
-                    cell["us"] = us
-
-                def turn_u(cell=cell):
-                    b = front_bank()
-                    nc.tensor.transpose(b[:, 0:P], cell["us"][:], ident[:])
-                    cell["ut"] = b
-
-                def add_u(q=q, cell=cell):
-                    t1 = pool.tile([P, P], F32, name="t1", tag="t1", bufs=2)
-                    nc.vector.tensor_scalar(
-                        out=t1[:], in0=cell["ut"][:, 0:P], scalar1=ESQ[c][:, q : q + 1], scalar2=None, op0=ALU.add
-                    )
-                    cell["t1"] = t1
-
-                def add_r(q=q, cell=cell):
+            def f0():
+                for u in (0, 1):
                     nc.vector.tensor_tensor(
-                        out=ST[c][:, q, 1 : NNEG + 1], in0=cell["R"][:, 0:P], in1=cell["t1"][:], op=ALU.add
+                        out=ST[cm][:, 2 * h + u, 1 : NNEG + 1], in0=RBANK[:, 256 * (k % 2) + P * u : 256 * (k % 2) + P * (u + 1)], in1=UT[2 * k + u][:],
+                        op=ALU.add,
                     )
 
-                def store():
-                    v = ST[c][:, 2 * h : 2 * h + 2, :]
-                    o = pool.tile([P, 2, NNEG + 1], F32, name="om", tag="om", bufs=2)
-                    nc.vector.tensor_scalar(out=v, in0=v, scalar1=0.0, scalar2=None, op0=ALU.max)
-                    nc.scalar.activation(out=o[:], in_=v, func=ACT.Sqrt)
-                    return o
+            def f1():
+                v = ST[cm][:, 2 * h : 2 * h + 2, :]
+                nc.vector.tensor_scalar(out=v, in0=v, scalar1=0.0, scalar2=None, op0=ALU.max)
 
-                for i in range(P):
-                    ops.append((lambda i=i, uop=uop: uop(i), [(1, reduce_u), (3, turn_u), (5, add_u)] if i == P - 1 else []))
-                ops.append((t3, []))
-                tail = [(1, add_r)]
-                if u == 1:
-                    cell2 = {}
+            later(s + 3, f0)
+            later(s + 4, f1)
+            store(cm, h, s + 5)
 
-                    def root(cell2=cell2, store=store):
-                        cell2["o"] = store()
-
-                    def neg(cell2=cell2):
-                        o = cell2["o"]
-                        nc.vector.tensor_scalar(out=o[:], in0=o[:], scalar1=-1.0, scalar2=None, op0=ALU.mult)
-                        t0 = 4 * c + 2 * h
-                        nc.sync.dma_start(out=out_view[:, t0 : t0 + 2, :], in_=o[:])
-
-                    tail = tail + [(2, root), (4, neg)]
-                for j in range(NNEG):
-                    ops.append((lambda j=j, rop=rop: rop(j), tail if j == NNEG - 1 else []))
-            return ops
-
-        BN = {}
-
-        def bn_bank(b, a, n):
-            for h in (0, 1):
-                nc.vector.bn_stats(
-                    out=BN[a][:, 2 * n + h, :], in_=b[:, 256 * h : 256 * (h + 1)].rearrange("p (b d) -> p d b", b=2)
-                )
-
-        def bn_post(a):
-            n = len(BN_J)
-            v = BN[a][:].rearrange("p g (b e) -> p (g b) e", e=3)
-            m2 = pool.tile([P, 4 * n], F32, name="m2", tag="m2", bufs=2)
-            nc.vector.tensor_tensor(out=m2[:], in0=v[:, :, 1], in1=v[:, :, 1], op=ALU.mult)
-            dst = ST[a][:, :, 1 + BN_J[0] : 2 + BN_J[-1] : BN_J[1] - BN_J[0]].rearrange("p q n -> p n q")
-            nc.vector.scalar_tensor_tensor(
-                out=dst, in0=m2[:].rearrange("p (n q) -> p n q", q=4), scalar=128.0,
-                in1=v[:, :, 2].rearrange("p (n q) -> p n q", q=4), op0=ALU.mult, op1=ALU.add,
-            )
-
-        OUTA = {}
-
-        def a_sqrt(a):
-            o = pool.tile([P, ROWS, NNEG + 1], F32, name="oa", tag="oa", bufs=2)
-            nc.scalar.activation(out=o[:], in_=ST[a][:], func=ACT.Sqrt)
-            OUTA[a] = o
-
-        def a_store(a):
-            o = OUTA[a]
-            nc.vector.tensor_scalar(out=o[:], in0=o[:], scalar1=-1.0, scalar2=None, op0=ALU.mult)
-            nc.sync.dma_start(out=out_view[:, ROWS * a : ROWS * (a + 1), :], in_=o[:])
-
-        def direct(s):
-            a = s // 128
-            j = s % 128
-            if j == 0:
-                BN[a] = pool.tile([P, 2 * len(BN_J), 6], F32, name="BN", tag="BN", bufs=2)
-            r = pool.tile([P, CW], F32, name="r", tag="r", bufs=4)
-            nc.vector.tensor_scalar(
-                out=r[:], in0=eT[a][:], scalar1=nTf[:, j : j + 1], scalar2=0.0, op0=ALU.subtract, op1=ALU.min
-            )
-            b = bank("tr", 3)
-            for q in range(ROWS):
-                nc.tensor.transpose(b[:, P * q : P * (q + 1)], r[:, P * q : P * (q + 1)], ident[:])
-            if j in BN_J:
-                later(s + 2, lambda b=b, a=a, n=BN_J.index(j): bn_bank(b, a, n))
-            else:
-                for q in range(ROWS):
-                    junk = pool.tile([P, P], BF16, name="junk", tag="junk", bufs=8)
-                    nc.scalar.activation(
-                        out=junk[:], in_=b[:, P * q : P * (q + 1)], func=ACT.Square, accum_out=ST[a][:, q, 1 + j : 2 + j]
-                    )
-            if j == 127:
-                later(s + 4, lambda a=a: bn_post(a))
-                later(s + 6, lambda a=a: a_sqrt(a))
-                later(s + 8, lambda a=a: a_store(a))
-
-        total = 512
-        head = 0
-        for s in range(total + 20):
+        for s in range(NG + 12):
             for fn in due.get(s, []):
                 fn()
-            if s in pieces:
-                run(pieces[s])
-            if s < total:
-                direct(s)
-            k = s // SLOT
-            o = s % SLOT
-            if k < 8:
-                make_planes(k, o)
-            if o == 0 and 1 <= k <= 8:
-                queue.extend(mask_ops(k - 1))
-            left = SLOT - o
-            if k > 8 or s >= total - 1:
-                left = 1
-            n = (len(queue) - head + left - 1) // left
-            for i in range(n):
-                fn, events = queue[head]
-                head += 1
-                fn()
-                for d, ev in events:
-                    later(s + d, ev)
+            run(pieces.get(s, []))
+            if s < NG:
+                planes(s)
+            if 1 <= s <= NG:
+                thins(s - 1, s)
+            if 2 <= s <= NG + 1:
+                adds(s - 2, s)
+                if WARM:
+                    dummy = front_bank()
+                    nc.tensor.matmul_mx(
+                        out=dummy[:], lhsT=wec[:].bitcast(FP8X4), lhsT_scale=wes[:],
+                        rhs=wc[:].bitcast(FP8X4), rhs_scale=ws[:], start=True, stop=True,
+                    )

@@ -24,8 +24,9 @@ CW = ROWS * P
 NCH = 4
 
 FLOPS = 2 * B * KV * KH + 2 * B * KH * D
-WARM = True
 FR = 3
+G = 16
+KICK = 8
 
 
 def tile_hypernymvisual_acc_t_kernel(
@@ -336,16 +337,18 @@ def tile_hypernymvisual_acc_t_kernel(
 
         pieces = {}
         for x in range(1, 4):
-            for c, start in ((x, 64 * x - 62), (x + 4, 64 * x - 61)):
+            for c in (x, x + 4):
                 for i, piece in enumerate(front(c)):
-                    pieces.setdefault(start + 2 * i, []).extend(piece)
+                    pieces.setdefault(32 * x - 31 + 29 * i // 20, []).extend(piece)
 
         due = {}
 
         def later(s, fn):
             due.setdefault(s, []).append(fn)
 
-        NG = 256
+        NG = 2048 // G
+        TG = 128 // G
+        JG = G // 2
         MD = {}
         SD = {}
         MI = {}
@@ -355,22 +358,23 @@ def tile_hypernymvisual_acc_t_kernel(
         RBANK = bank("R", 1)
 
         def planes(g):
-            tile = g // 16
+            tile = g // TG
             c = tile // 4
-            d0 = 8 * (g % 16)
-            k = g // 32
+            d0 = G * (g % TG)
+            k = g // (2 * TG)
             cm = NCH + k // 2
-            i0 = 256 * (k % 2) + 8 * (g % 32)
-            j0 = 4 * (g % 32)
-            md = pool.tile([P, 8, NNEG], BF16, name="md", tag="md", bufs=3)
-            sd = pool.tile([P, 8, NNEG], F32, name="sd", tag="sd", bufs=3)
-            mi = pool.tile([P, 8, NNEG], BF16, name="mi", tag="mi", bufs=3)
-            mj = pool.tile([P, 4, 256], BF16, name="mj", tag="mj", bufs=3)
+            i0 = 256 * (k % 2) + G * (g % (2 * TG))
+            j0 = JG * (g % (2 * TG))
+            md = pool.tile([P, G, NNEG], BF16, name="md", tag="md", bufs=3)
+            sd = pool.tile([P, G, NNEG], F32, name="sd", tag="sd", bufs=3)
+            mi = pool.tile([P, G, NNEG], BF16, name="mi", tag="mi", bufs=3)
+            mj = pool.tile([P, JG, 256], BF16, name="mj", tag="mj", bufs=3)
             MD[g] = md
             SD[g] = sd
             MI[g] = mi
             MJ[g] = mj
-            for x in range(8):
+            h = 256 * (k % 2)
+            for x in range(G):
                 col = D * (tile % 4) + d0 + x
                 nc.vector.tensor_scalar(
                     out=md[:, x, :], in0=NB[:, d0 + x, :], scalar1=E[c][:, col : col + 1], scalar2=None, op0=ALU.max
@@ -378,26 +382,25 @@ def tile_hypernymvisual_acc_t_kernel(
                 nc.scalar.activation(
                     out=sd[:, x, :], in_=md[:, x, :], func=ACT.Square, bias=E[c][:, col : col + 1], scale=-1.0
                 )
-            for x in range(8):
                 nc.vector.tensor_scalar(
                     out=mi[:, x, :], in0=nT[:], scalar1=eT[cm][:, i0 + x : i0 + x + 1], scalar2=None, op0=ALU.max
                 )
-            h = 256 * (k % 2)
-            for x in range(4):
-                nc.vector.tensor_scalar(
-                    out=mj[:, x, :], in0=eB[cm][:, h : h + 256], scalar1=nTf[:, j0 + x : j0 + x + 1], scalar2=None, op0=ALU.max
-                )
+                if x % 2 == 1:
+                    y = x // 2
+                    nc.vector.tensor_scalar(
+                        out=mj[:, y, :], in0=eB[cm][:, h : h + 256], scalar1=nTf[:, j0 + y : j0 + y + 1], scalar2=None, op0=ALU.max
+                    )
 
         def adds(g, s):
-            tile = g // 16
-            if g % 16 == 0:
+            tile = g // TG
+            if g % TG == 0:
                 ACC[tile] = bank("acc", 2)
-            for x in range(8):
+            for x in range(G):
                 nc.tensor.matmul(
                     ACC[tile][:, 0:P], lhsT=SD[g][:, x, :], rhs=ident[:], is_transpose=True,
-                    start=(g % 16 == 0 and x == 0), stop=(g % 16 == 15 and x == 7),
+                    start=(g % TG == 0 and x == 0), stop=(g % TG == TG - 1 and x == G - 1),
                 )
-            if g % 16 == 15:
+            if g % TG == TG - 1:
                 finish_direct(tile, s)
 
         def finish_direct(tile, s):
@@ -444,33 +447,36 @@ def tile_hypernymvisual_acc_t_kernel(
             later(s, f0)
             later(s + 1, f1)
 
-        def thins(g, s):
-            k = g // 32
+        def thins_i(g, s):
+            k = g // (2 * TG)
             cm = NCH + k // 2
-            u = (g % 32) // 16
+            u = (g % (2 * TG)) // TG
             q = 2 * (k % 2) + u
-            if g % 16 == 0:
-                UB[g // 16] = bank("U", 2)
-            ub = UB[g // 16]
-            for x in range(8):
-                i = 8 * (g % 16) + x
+            if g % TG == 0:
+                UB[g // TG] = bank("U", 2)
+            ub = UB[g // TG]
+            for x in range(G):
+                i = G * (g % TG) + x
                 nc.tensor.matmul(
                     ub[:, 2 * i : 2 * i + 2], lhsT=MI[g][:, x, :], rhs=GL[cm][:, :, P * q + i], start=True, stop=True
                 )
-            if g % 16 == 15:
+            if g % TG == TG - 1:
                 nc.tensor.matmul(
                     ub[:, 256:384], lhsT=nT[:], rhs=GL[cm][:, 0, P * q : P * (q + 1)], start=True, stop=True
                 )
-                finish_u(k, u, g // 16, s)
+                finish_u(k, u, g // TG, s)
+
+        def thins_j(g, s):
+            k = g // (2 * TG)
             rb = RBANK[:, 256 * (k % 2) : 256 * (k % 2 + 1)]
-            for x in range(4):
-                j = 4 * (g % 32) + x
+            for x in range(JG):
+                j = JG * (g % (2 * TG)) + x
                 for v in (0, 1):
                     nc.tensor.matmul(
                         rb[:, P * v + j : P * v + j + 1], lhsT=MJ[g][:, x, P * v : P * (v + 1)], rhs=nT[:, j : j + 1],
                         start=True, stop=True,
                     )
-            if g % 32 == 31:
+            if g % (2 * TG) == 2 * TG - 1:
                 finish_r(k, s)
 
         UT = {}
@@ -524,6 +530,15 @@ def tile_hypernymvisual_acc_t_kernel(
             later(s + 4, f1)
             store(cm, h, s + 5)
 
+        def warm():
+            dummy = front_bank()
+            nc.tensor.matmul_mx(
+                out=dummy[:], lhsT=wec[:].bitcast(FP8X4), lhsT_scale=wes[:],
+                rhs=wc[:].bitcast(FP8X4), rhs_scale=ws[:], start=True, stop=True,
+            )
+
+        for i in range(KICK):
+            warm()
         for s in range(NG + 12):
             for fn in due.get(s, []):
                 fn()
@@ -531,12 +546,10 @@ def tile_hypernymvisual_acc_t_kernel(
             if s < NG:
                 planes(s)
             if 1 <= s <= NG:
-                thins(s - 1, s)
+                thins_i(s - 1, s)
+                warm()
+                thins_j(s - 1, s)
+                warm()
             if 2 <= s <= NG + 1:
                 adds(s - 2, s)
-                if WARM:
-                    dummy = front_bank()
-                    nc.tensor.matmul_mx(
-                        out=dummy[:], lhsT=wec[:].bitcast(FP8X4), lhsT_scale=wes[:],
-                        rhs=wc[:].bitcast(FP8X4), rhs_scale=ws[:], start=True, stop=True,
-                    )
+                warm()

@@ -143,10 +143,7 @@ def tile_hypernymvisual_acc_t_kernel(
             for i in range(8):
                 d = 8 * x + i
                 nc.tensor.transpose(b[:, i, :], nn[:, d : d + 1].to_broadcast([P, P]), ident_b[:])
-            if x % 2:
-                nc.vector.tensor_copy(out=NB[:, 8 * x : 8 * x + 8, :], in_=b[:])
-            else:
-                nc.scalar.copy(out=NB[:, 8 * x : 8 * x + 8, :], in_=b[:])
+            nc.scalar.copy(out=NB[:, 8 * x : 8 * x + 8, :], in_=b[:])
 
         E = {}
         eT = {}
@@ -224,6 +221,9 @@ def tile_hypernymvisual_acc_t_kernel(
                     t = pool.tile([P, CW], F32, name="eT", tag="eT", bufs=2)
                     nc.scalar.activation(out=t[:], in_=st["e"][:], func=ACT.Identity, bias=be[:])
                     eT[c] = t
+                    h = pool.tile([P, CW], BF16, name="eB", tag="eB", bufs=2)
+                    nc.scalar.activation(out=h[:], in_=st["e"][:], func=ACT.Identity, bias=be[:])
+                    eB[c] = h
                 else:
                     t = pool.tile([P, CW], F32, name="E", tag="E", bufs=2)
                     nc.vector.tensor_tensor(
@@ -235,9 +235,6 @@ def tile_hypernymvisual_acc_t_kernel(
 
             def eback():
                 if thin:
-                    t = pool.tile([P, CW], BF16, name="eB", tag="eB", bufs=2)
-                    nc.vector.tensor_copy(out=t[:], in_=eT[c][:])
-                    eB[c] = t
                     b = front_bank()
                     for q in range(ROWS):
                         r = slice(P * q, P * (q + 1))
@@ -256,47 +253,43 @@ def tile_hypernymvisual_acc_t_kernel(
                     GL[c] = g
 
             def rows_a():
-                h = pool.tile([P, CW], BF16, name="er", tag="er", bufs=2)
-                nc.vector.tensor_copy(out=h[:], in_=st["eb"][:])
                 t = pool.tile([P, CW], F32, name="xp", tag="xp", bufs=2)
                 nc.vector.tensor_tensor(out=t[:], in0=pp[:, CW * c : CW * (c + 1)], in1=st["eb"][:], op=ALU.subtract)
                 st["xp"] = t
                 s = pool.tile([P, ROWS, NNEG + 1], F32, name="ST", tag="ST", bufs=4)
                 ST[c] = s
-                d = pool.tile([P, CW], F32, name="ed", tag="ed", bufs=2)
-                nc.vector.tensor_tensor(out=d[:], in0=h[:], in1=st["eb"][:], op=ALU.subtract)
-                st["ed"] = d
+                if not thin:
+                    h = pool.tile([P, CW], BF16, name="er", tag="er", bufs=2)
+                    nc.scalar.copy(out=h[:], in_=E[c][:])
+                    st["er"] = h
 
-            def rows_b():
-                q2 = pool.tile([P, 2, ROWS], F32, name="q2", tag="q2", bufs=2)
+            def square_sums(src, dst):
                 for q in range(ROWS):
                     junk = pool.tile([P, P], BF16, name="junk", tag="junk", bufs=4)
-                    nc.scalar.activation(
-                        out=junk[:], in_=st["ed"][:, P * q : P * (q + 1)], func=ACT.Square, accum_out=q2[:, 0, q : q + 1]
-                    )
+                    nc.scalar.activation(out=junk[:], in_=src[:, P * q : P * (q + 1)], func=ACT.Square, accum_out=dst[q])
+
+            def rows_b():
+                x = st["xp"]
+                nc.vector.tensor_scalar(out=x[:], in0=x[:], scalar1=0.0, scalar2=None, op0=ALU.max)
+                r = pool.tile([P, ROWS], F32, name="rowc", tag="rowc", bufs=4)
+                ROWC[c] = r
+                cols = [r[:, q : q + 1] for q in range(ROWS)]
                 if thin:
-                    for q in range(ROWS):
-                        junk = pool.tile([P, P], BF16, name="junk", tag="junk", bufs=4)
-                        nc.scalar.activation(
-                            out=junk[:], in_=st["eb"][:, P * q : P * (q + 1)], func=ACT.Square, accum_out=q2[:, 1, q : q + 1]
-                        )
-                st["q2"] = q2
+                    square_sums(st["eb"], cols)
+                else:
+                    d = pool.tile([P, CW], F32, name="ed", tag="ed", bufs=2)
+                    nc.vector.tensor_tensor(out=d[:], in0=st["er"][:], in1=E[c][:], op=ALU.subtract)
+                    st["ed"] = d
 
             def rows_c():
-                q2 = st["q2"]
-                r = pool.tile([P, ROWS], F32, name="rowc", tag="rowc", bufs=4)
-                if thin:
-                    nc.vector.tensor_tensor(out=r[:], in0=q2[:, 1, :], in1=q2[:, 0, :], op=ALU.subtract)
-                else:
-                    nc.vector.tensor_scalar(out=r[:], in0=q2[:, 0, :], scalar1=-1.0, scalar2=None, op0=ALU.mult)
-                ROWC[c] = r
+                if not thin:
+                    r = ROWC[c]
+                    square_sums(st["ed"], [r[:, q : q + 1] for q in range(ROWS)])
+                square_sums(st["xp"], [ST[c][:, q, 0:1] for q in range(ROWS)])
 
-            def psum2(q):
-                j2 = pool.tile([P, P], F32, name="junkp", tag="junkp", bufs=2)
-                x = st["xp"][:, P * q : P * (q + 1)]
-                nc.vector.scalar_tensor_tensor(
-                    out=j2[:], in0=x, scalar=0.0, in1=x, op0=ALU.max, op1=ALU.mult, accum_out=ST[c][:, q, 0:1]
-                )
+            def rows_d():
+                if not thin:
+                    nc.vector.tensor_scalar(out=ROWC[c][:], in0=ROWC[c][:], scalar1=-1.0, scalar2=None, op0=ALU.mult)
 
             return [
                 [lambda: widen(0)],
@@ -317,8 +310,8 @@ def tile_hypernymvisual_acc_t_kernel(
                 [eback],
                 [rows_a],
                 [rows_b, split_b],
-                [rows_c, lambda: psum2(0), lambda: psum2(1)],
-                [lambda: psum2(2), lambda: psum2(3)],
+                [rows_c],
+                [rows_d],
             ]
 
         def run(piece):
@@ -374,22 +367,23 @@ def tile_hypernymvisual_acc_t_kernel(
             MI[g] = mi
             MJ[g] = mj
             h = 256 * (k % 2)
+            col = D * (tile % 4) + d0
             for x in range(G):
-                col = D * (tile % 4) + d0 + x
                 nc.vector.tensor_scalar(
-                    out=md[:, x, :], in0=NB[:, d0 + x, :], scalar1=E[c][:, col : col + 1], scalar2=None, op0=ALU.max
+                    out=md[:, x, :], in0=NB[:, d0 + x, :], scalar1=E[c][:, col + x : col + x + 1], scalar2=None, op0=ALU.max
                 )
+            for x in reversed(range(G)):
                 nc.scalar.activation(
-                    out=sd[:, x, :], in_=md[:, x, :], func=ACT.Square, bias=E[c][:, col : col + 1], scale=-1.0
+                    out=sd[:, x, :], in_=md[:, x, :], func=ACT.Square, bias=E[c][:, col + x : col + x + 1], scale=-1.0
                 )
+            for x in range(G):
                 nc.vector.tensor_scalar(
                     out=mi[:, x, :], in0=nT[:], scalar1=eT[cm][:, i0 + x : i0 + x + 1], scalar2=None, op0=ALU.max
                 )
-                if x % 2 == 1:
-                    y = x // 2
-                    nc.vector.tensor_scalar(
-                        out=mj[:, y, :], in0=eB[cm][:, h : h + 256], scalar1=nTf[:, j0 + y : j0 + y + 1], scalar2=None, op0=ALU.max
-                    )
+            for y in range(JG):
+                nc.vector.tensor_scalar(
+                    out=mj[:, y, :], in0=eB[cm][:, h : h + 256], scalar1=nTf[:, j0 + y : j0 + y + 1], scalar2=None, op0=ALU.max
+                )
 
         def adds(g, s):
             tile = g // TG
@@ -419,9 +413,8 @@ def tile_hypernymvisual_acc_t_kernel(
                 cell["b"] = b
 
             def f2():
-                nc.vector.tensor_scalar(
-                    out=ST[c][:, q, 1 : NNEG + 1], in0=cell["b"][:, 0:P], scalar1=ROWC[c][:, q : q + 1], scalar2=0.0,
-                    op0=ALU.add, op1=ALU.max,
+                nc.scalar.activation(
+                    out=ST[c][:, q, 1 : NNEG + 1], in_=cell["b"][:, 0:P], func=ACT.Relu, bias=ROWC[c][:, q : q + 1]
                 )
 
             later(s + 1, f0)
@@ -455,7 +448,7 @@ def tile_hypernymvisual_acc_t_kernel(
             if g % TG == 0:
                 UB[g // TG] = bank("U", 2)
             ub = UB[g // TG]
-            for x in range(G):
+            for x in reversed(range(G)):
                 i = G * (g % TG) + x
                 nc.tensor.matmul(
                     ub[:, 2 * i : 2 * i + 2], lhsT=MI[g][:, x, :], rhs=GL[cm][:, :, P * q + i], start=True, stop=True
@@ -469,7 +462,7 @@ def tile_hypernymvisual_acc_t_kernel(
         def thins_j(g, s):
             k = g // (2 * TG)
             rb = RBANK[:, 256 * (k % 2) : 256 * (k % 2 + 1)]
-            for x in range(JG):
+            for x in reversed(range(JG)):
                 j = JG * (g % (2 * TG)) + x
                 for v in (0, 1):
                     nc.tensor.matmul(
@@ -502,9 +495,7 @@ def tile_hypernymvisual_acc_t_kernel(
 
             def f2():
                 t1 = pool.tile([P, P], F32, name="t1", tag="t1", bufs=4)
-                nc.vector.tensor_scalar(
-                    out=t1[:], in0=cell["b"][:, 0:P], scalar1=ROWC[cm][:, q : q + 1], scalar2=None, op0=ALU.add
-                )
+                nc.scalar.activation(out=t1[:], in_=cell["b"][:, 0:P], func=ACT.Identity, bias=ROWC[cm][:, q : q + 1])
                 UT[2 * k + u] = t1
 
             later(s + 1, f0)

@@ -24,9 +24,9 @@ CW = ROWS * P
 NCH = 4
 
 FLOPS = 2 * B * KV * KH + 2 * B * KH * D
-FR = 3
+FR = 2
 G = 16
-KICK = 8
+PAIRS = 4
 
 
 def tile_hypernymvisual_acc_t_kernel(
@@ -102,6 +102,18 @@ def tile_hypernymvisual_acc_t_kernel(
             else:
                 nc.scalar.copy(out=dst, in_=srcv)
 
+        NB = keep.tile([P, D, NNEG], BF16, name="NB")
+
+        def spread(x):
+            b = psum.tile([P, 8, P], BF16, name="fr", tag="fr", bufs=FR)
+            for i in range(8):
+                d = 8 * x + i
+                nc.tensor.transpose(b[:, i, :], nn[:, d : d + 1].to_broadcast([P, P]), ident_b[:])
+            nc.scalar.copy(out=NB[:, 8 * x : 8 * x + 8, :], in_=b[:])
+
+        for x in range(6):
+            spread(x)
+
         wg = pool.tile([P, 4 * CW], BF16, name="xg", tag="xg", bufs=2, align_bytes=64)
         b0 = turn_pe(wh, 0)
         b1 = turn_pe(wh, 1)
@@ -135,15 +147,6 @@ def tile_hypernymvisual_acc_t_kernel(
         nc.vector.tensor_copy(out=be[:], in_=be_raw[:])
         bew = keep.tile([P, 1, D], F32, name="bew")
         nc.vector.tensor_copy(out=bew[:, 0, :], in_=bew_raw[:])
-
-        NB = keep.tile([P, D, NNEG], BF16, name="NB")
-
-        def spread(x):
-            b = psum.tile([P, 8, P], BF16, name="fr", tag="fr", bufs=FR)
-            for i in range(8):
-                d = 8 * x + i
-                nc.tensor.transpose(b[:, i, :], nn[:, d : d + 1].to_broadcast([P, P]), ident_b[:])
-            nc.scalar.copy(out=NB[:, 8 * x : 8 * x + 8, :], in_=b[:])
 
         E = {}
         eT = {}
@@ -322,8 +325,8 @@ def tile_hypernymvisual_acc_t_kernel(
         fm = front(4)
         for i in range(len(fd)):
             run(fd[i])
-            if i < 16:
-                spread(i)
+            if i < 10:
+                spread(6 + i)
             run(fm[i])
         for c in order[2:]:
             load_raw(c)
@@ -341,14 +344,15 @@ def tile_hypernymvisual_acc_t_kernel(
 
         NG = 2048 // G
         TG = 128 // G
-        JG = G // 2
+        CG = 4 * TG
+        JG = NNEG // CG
         MD = {}
         SD = {}
         MI = {}
         MJ = {}
         ACC = {}
         UB = {}
-        RBANK = bank("R", 1)
+        RB = {}
 
         def planes(g):
             tile = g // TG
@@ -357,42 +361,50 @@ def tile_hypernymvisual_acc_t_kernel(
             k = g // (2 * TG)
             cm = NCH + k // 2
             i0 = 256 * (k % 2) + G * (g % (2 * TG))
-            j0 = JG * (g % (2 * TG))
+            j0 = JG * (g % CG)
             md = pool.tile([P, G, NNEG], BF16, name="md", tag="md", bufs=3)
-            sd = pool.tile([P, G, NNEG], F32, name="sd", tag="sd", bufs=3)
-            mi = pool.tile([P, G, NNEG], BF16, name="mi", tag="mi", bufs=3)
-            mj = pool.tile([P, JG, 256], BF16, name="mj", tag="mj", bufs=3)
+            sd = pool.tile([P, G, NNEG], F32, name="sd", tag="sd", bufs=4)
+            mi = pool.tile([P, G, NNEG], BF16, name="mi", tag="mi", bufs=4)
+            mj = pool.tile([P, JG, CW], BF16, name="mj", tag="mj", bufs=4)
             MD[g] = md
             SD[g] = sd
             MI[g] = mi
             MJ[g] = mj
-            h = 256 * (k % 2)
             col = D * (tile % 4) + d0
             for x in range(G):
                 nc.vector.tensor_scalar(
                     out=md[:, x, :], in0=NB[:, d0 + x, :], scalar1=E[c][:, col + x : col + x + 1], scalar2=None, op0=ALU.max
                 )
-            for x in reversed(range(G)):
                 nc.scalar.activation(
                     out=sd[:, x, :], in_=md[:, x, :], func=ACT.Square, bias=E[c][:, col + x : col + x + 1], scale=-1.0
                 )
-            for x in range(G):
                 nc.vector.tensor_scalar(
                     out=mi[:, x, :], in0=nT[:], scalar1=eT[cm][:, i0 + x : i0 + x + 1], scalar2=None, op0=ALU.max
                 )
-            for y in range(JG):
-                nc.vector.tensor_scalar(
-                    out=mj[:, y, :], in0=eB[cm][:, h : h + 256], scalar1=nTf[:, j0 + y : j0 + y + 1], scalar2=None, op0=ALU.max
-                )
+                if x % 4 == 3:
+                    y = x // 4
+                    nc.vector.tensor_scalar(
+                        out=mj[:, y, :], in0=eB[cm][:], scalar1=nTf[:, j0 + y : j0 + y + 1], scalar2=None, op0=ALU.max
+                    )
+
+        SP = {}
+
+        def pair_adds(g):
+            sp = pool.tile([P, PAIRS, NNEG], F32, name="sp", tag="sp", bufs=3)
+            nc.vector.tensor_tensor(
+                out=sp[:], in0=SD[g][:, 0:PAIRS, :], in1=SD[g][:, PAIRS : 2 * PAIRS, :], op=ALU.add
+            )
+            SP[g] = sp
 
         def adds(g, s):
             tile = g // TG
             if g % TG == 0:
                 ACC[tile] = bank("acc", 2)
-            for x in range(G):
+            blocks = [SP[g][:, x, :] for x in range(PAIRS)] + [SD[g][:, x, :] for x in range(2 * PAIRS, G)]
+            for x in range(len(blocks)):
                 nc.tensor.matmul(
-                    ACC[tile][:, 0:P], lhsT=SD[g][:, x, :], rhs=ident[:], is_transpose=True,
-                    start=(g % TG == 0 and x == 0), stop=(g % TG == TG - 1 and x == G - 1),
+                    ACC[tile][:, 0:P], lhsT=blocks[x], rhs=ident[:], is_transpose=True,
+                    start=(g % TG == 0 and x == 0), stop=(g % TG == TG - 1 and x == len(blocks) - 1),
                 )
             if g % TG == TG - 1:
                 finish_direct(tile, s)
@@ -408,20 +420,18 @@ def tile_hypernymvisual_acc_t_kernel(
                 cell["t"] = t
 
             def f1():
-                b = front_bank()
-                nc.tensor.transpose(b[:, 0:P], cell["t"][:], ident[:])
-                cell["b"] = b
+                nc.tensor.transpose(ACC[tile][:, P : 2 * P], cell["t"][:], ident[:])
 
             def f2():
                 nc.scalar.activation(
-                    out=ST[c][:, q, 1 : NNEG + 1], in_=cell["b"][:, 0:P], func=ACT.Relu, bias=ROWC[c][:, q : q + 1]
+                    out=ST[c][:, q, 1 : NNEG + 1], in_=ACC[tile][:, P : 2 * P], func=ACT.Relu, bias=ROWC[c][:, q : q + 1]
                 )
 
-            later(s + 1, f0)
-            later(s + 2, f1)
-            later(s + 3, f2)
+            later(s + 2, f0)
+            later(s + 3, f1)
+            later(s + 4, f2)
             if q % 2:
-                store(c, q // 2, s + 4)
+                store(c, q // 2, s + 5)
 
         def store(c, h, s):
             cell = {}
@@ -448,7 +458,7 @@ def tile_hypernymvisual_acc_t_kernel(
             if g % TG == 0:
                 UB[g // TG] = bank("U", 2)
             ub = UB[g // TG]
-            for x in reversed(range(G)):
+            for x in range(G):
                 i = G * (g % TG) + x
                 nc.tensor.matmul(
                     ub[:, 2 * i : 2 * i + 2], lhsT=MI[g][:, x, :], rhs=GL[cm][:, :, P * q + i], start=True, stop=True
@@ -460,17 +470,19 @@ def tile_hypernymvisual_acc_t_kernel(
                 finish_u(k, u, g // TG, s)
 
         def thins_j(g, s):
-            k = g // (2 * TG)
-            rb = RBANK[:, 256 * (k % 2) : 256 * (k % 2 + 1)]
-            for x in reversed(range(JG)):
-                j = JG * (g % (2 * TG)) + x
-                for v in (0, 1):
+            m = g // CG
+            if g % CG == 0:
+                RB[m] = bank("R", 2)
+            rb = RB[m]
+            for x in range(JG):
+                j = JG * (g % CG) + x
+                for v in range(ROWS):
                     nc.tensor.matmul(
                         rb[:, P * v + j : P * v + j + 1], lhsT=MJ[g][:, x, P * v : P * (v + 1)], rhs=nT[:, j : j + 1],
                         start=True, stop=True,
                     )
-            if g % (2 * TG) == 2 * TG - 1:
-                finish_r(k, s)
+            if g % CG == CG - 1:
+                finish_r(m, s)
 
         UT = {}
 
@@ -489,47 +501,35 @@ def tile_hypernymvisual_acc_t_kernel(
                 cell["t"] = t2
 
             def f1():
-                b = front_bank()
-                nc.tensor.transpose(b[:, 0:P], cell["t"][:], ident[:])
-                cell["b"] = b
+                nc.tensor.transpose(UB[key][:, 384:512], cell["t"][:], ident[:])
 
             def f2():
-                t1 = pool.tile([P, P], F32, name="t1", tag="t1", bufs=4)
-                nc.scalar.activation(out=t1[:], in_=cell["b"][:, 0:P], func=ACT.Identity, bias=ROWC[cm][:, q : q + 1])
-                UT[2 * k + u] = t1
+                t1 = pool.tile([P, P], F32, name="t1", tag="t1", bufs=6)
+                nc.scalar.activation(out=t1[:], in_=UB[key][:, 384:512], func=ACT.Identity, bias=ROWC[cm][:, q : q + 1])
+                UT[key] = t1
 
-            later(s + 1, f0)
-            later(s + 2, f1)
-            later(s + 3, f2)
+            later(s + 2, f0)
+            later(s + 3, f1)
+            later(s + 4, f2)
 
-        def finish_r(k, s):
-            cm = NCH + k // 2
-            h = k % 2
+        def finish_r(m, s):
+            cm = NCH + m
 
             def f0():
-                for u in (0, 1):
+                for q in range(ROWS):
                     nc.vector.tensor_tensor(
-                        out=ST[cm][:, 2 * h + u, 1 : NNEG + 1], in0=RBANK[:, 256 * (k % 2) + P * u : 256 * (k % 2) + P * (u + 1)], in1=UT[2 * k + u][:],
+                        out=ST[cm][:, q, 1 : NNEG + 1], in0=RB[m][:, P * q : P * (q + 1)], in1=UT[ROWS * m + q][:],
                         op=ALU.add,
                     )
 
             def f1():
-                v = ST[cm][:, 2 * h : 2 * h + 2, :]
-                nc.vector.tensor_scalar(out=v, in0=v, scalar1=0.0, scalar2=None, op0=ALU.max)
+                nc.vector.tensor_scalar(out=ST[cm][:], in0=ST[cm][:], scalar1=0.0, scalar2=None, op0=ALU.max)
 
-            later(s + 3, f0)
-            later(s + 4, f1)
-            store(cm, h, s + 5)
+            later(s + 5, f0)
+            later(s + 6, f1)
+            store(cm, 0, s + 7)
+            store(cm, 1, s + 7)
 
-        def warm():
-            dummy = front_bank()
-            nc.tensor.matmul_mx(
-                out=dummy[:], lhsT=wec[:].bitcast(FP8X4), lhsT_scale=wes[:],
-                rhs=wc[:].bitcast(FP8X4), rhs_scale=ws[:], start=True, stop=True,
-            )
-
-        for i in range(KICK):
-            warm()
         for s in range(NG + 12):
             for fn in due.get(s, []):
                 fn()
@@ -537,10 +537,11 @@ def tile_hypernymvisual_acc_t_kernel(
             if s < NG:
                 planes(s)
             if 1 <= s <= NG:
-                thins_i(s - 1, s)
-                warm()
-                thins_j(s - 1, s)
-                warm()
-            if 2 <= s <= NG + 1:
+                pair_adds(s - 1)
+            if s % 2 and 2 <= s <= NG + 1:
                 adds(s - 2, s)
-                warm()
+            if 1 <= s <= NG:
+                thins_i(s - 1, s)
+                thins_j(s - 1, s)
+            if s % 2 == 0 and 2 <= s <= NG + 1:
+                adds(s - 2, s)

from contextlib import ExitStack

import concourse.mybir as mybir
from concourse.masks import make_identity

F32 = mybir.dt.float32
BF16 = mybir.dt.bfloat16
U32 = mybir.dt.uint32
U8 = mybir.dt.uint8
FP8 = mybir.dt.float8_e4m3fn
FP8X4 = mybir.dt.float8_e4m3fn_x4
ALU = mybir.AluOpType
ACT = mybir.ActivationFunctionType
AX = mybir.AxisListType

P = 128
B = 4096
KV = 512
KH = 512
D = 128
NNEG = 128
ROWS = 4
CW = ROWS * P
NCH = 4

FLOPS = 2 * B * KV * KH + 2 * B * KH * D
FR = 2
G = 16
PAIRS = 4


def tile_hypernymvisual_acc_t_kernel(
    tc, vfs_bytes, vfs_scale, p_lfs, n_lfs, W_hidden, b_hidden, W_embed, b_embed, out
):
    nc = tc.nc
    with ExitStack() as ctx:
        ctx.enter_context(tc.manual_schedule())
        keep = ctx.enter_context(tc.tile_pool(name="keep", bufs=1))
        pool = ctx.enter_context(tc.tile_pool(name="work", bufs=2))
        psum = ctx.enter_context(tc.psum_pool(name="psum", bufs=1))

        xb_view = vfs_bytes.rearrange("(p c q) k -> c p (q k)", c=8, q=ROWS)
        out_view = out.rearrange("(p t) n -> p t n", t=32)

        order = [0, 4, 1, 5, 2, 6, 3, 7]
        raw = {}

        def load_raw(c):
            t = pool.tile([P, ROWS * KV], U8, name="raw", tag="raw", bufs=4)
            nc.sync.dma_start(out=t[:], in_=xb_view[c])
            raw[c] = t

        nn = keep.tile([P, D], BF16, name="nn", align_bytes=64)
        nc.sync.dma_start(out=nn[:], in_=n_lfs)
        wh = pool.tile([P, ROWS * KV], BF16, name="wide", tag="wide", bufs=2, align_bytes=64)
        nc.sync.dma_start(out=wh[:].rearrange("p (t k) -> p t k", t=4), in_=W_hidden.rearrange("(m t) k -> m t k", t=4))
        scale = keep.tile([P, KV], F32, name="scale")
        nc.scalar.dma_start(out=scale[:], in_=vfs_scale.rearrange("o k -> (o k)").partition_broadcast(P))
        load_raw(0)
        load_raw(4)
        we = keep.tile([P, KH], BF16, name="we", align_bytes=64)
        nc.sync.dma_start(out=we[:], in_=W_embed)
        bh_raw = keep.tile([P, 4], BF16, name="bh_raw")
        nc.scalar.dma_start(out=bh_raw[:], in_=b_hidden.rearrange("(m t) -> m t", t=4))
        be_raw = keep.tile([P, 1], BF16, name="be_raw")
        nc.scalar.dma_start(out=be_raw[:], in_=b_embed.rearrange("(d o) -> d o", o=1))
        bew_raw = keep.tile([P, D], BF16, name="bew_raw")
        nc.scalar.dma_start(out=bew_raw[:], in_=b_embed.partition_broadcast(P))
        pp = keep.tile([P, 32 * D], BF16, name="pp")
        nc.sync.dma_start(out=pp[:].rearrange("p (t d) -> p t d", t=32), in_=p_lfs.rearrange("(p t) d -> p t d", t=32))

        one = keep.tile([P, 1], F32, name="one")
        nc.vector.memset(one[:], 1.0)
        one_out = keep.tile([P, 1], F32, name="one_out")
        nc.scalar.activation(out=one_out[:], in_=one[:], func=ACT.Sqrt)
        ident = keep.tile([P, P], F32, name="ident")
        make_identity(nc, ident[:])
        ident_b = keep.tile([P, P], BF16, name="ident_b")
        nc.vector.tensor_copy(out=ident_b[:], in_=ident[:])

        def bank(tag, bufs):
            t = psum.tile([P, 512], F32, name=tag, tag=tag, bufs=bufs)
            return t

        def front_bank():
            return bank("fr", FR)

        def turn_pe(src, half):
            words = src[:].bitcast(F32)
            b = front_bank()
            for q in (2 * half, 2 * half + 1):
                for u in (0, 1):
                    lo = 256 * (q % 2) + 128 * u
                    nc.tensor.transpose(b[:, lo : lo + 128], words[:, 256 * q + u : 256 * (q + 1) : 2], ident[:])
            return b

        def turn_copy(b, grouped, half, eng):
            dst = grouped[:].bitcast(F32)[:, 512 * half : 512 * (half + 1)].rearrange("p (q r u) -> p q r u", q=2, u=2)
            srcv = b[:].rearrange("p (q u r) -> p q r u", q=2, u=2)
            if eng == "v":
                nc.vector.tensor_copy(out=dst, in_=srcv)
            else:
                nc.scalar.copy(out=dst, in_=srcv)

        NB = keep.tile([P, D, NNEG], BF16, name="NB")

        def spread(x):
            b = psum.tile([P, 8, P], BF16, name="fr", tag="fr", bufs=FR)
            for i in range(8):
                d = 8 * x + i
                nc.tensor.transpose(b[:, i, :], nn[:, d : d + 1].to_broadcast([P, P]), ident_b[:])
            nc.scalar.copy(out=NB[:, 8 * x : 8 * x + 8, :], in_=b[:])

        for x in range(6):
            spread(x)

        wg = pool.tile([P, 4 * CW], BF16, name="xg", tag="xg", bufs=2, align_bytes=64)
        b0 = turn_pe(wh, 0)
        b1 = turn_pe(wh, 1)
        turn_copy(b0, wg, 0, "v")
        turn_copy(b1, wg, 1, "s")
        wc = keep.tile([P, CW], U32, name="wc", align_bytes=64)
        ws = keep.tile([P, CW], U8, name="ws", align_bytes=64)
        nc.vector.quantize_mx(out=wc[:].bitcast(FP8X4), scales=ws[:], in_=wg[:])

        web = front_bank()
        for u in (0, 1):
            nc.tensor.transpose(web[:, 128 * u : 128 * (u + 1)], we[:].bitcast(F32)[:, u::2], ident[:])
        weg = keep.tile([P, 4 * D], BF16, name="weg", align_bytes=64)
        nc.scalar.copy(
            out=weg[:].bitcast(F32).rearrange("p (r u) -> p r u", u=2),
            in_=web[:, 0:256].rearrange("p (u r) -> p r u", u=2),
        )
        wec = keep.tile([P, D], U32, name="wec", align_bytes=64)
        wes = keep.tile([P, D], U8, name="wes", align_bytes=64)
        nc.vector.quantize_mx(out=wec[:].bitcast(FP8X4), scales=wes[:], in_=weg[:])

        nb = psum.tile([P, D], BF16, name="fr", tag="fr", bufs=FR)
        nc.tensor.transpose(nb[:], nn[:], ident_b[:])
        nT = keep.tile([P, NNEG], BF16, name="nT")
        nc.vector.tensor_copy(out=nT[:], in_=nb[:])
        nTf = keep.tile([P, NNEG], F32, name="nTf")
        nc.vector.tensor_copy(out=nTf[:], in_=nT[:])
        bh = keep.tile([P, 1, 4], F32, name="bh")
        nc.vector.tensor_copy(out=bh[:, 0, :], in_=bh_raw[:])
        be = keep.tile([P, 1], F32, name="be")
        nc.vector.tensor_copy(out=be[:], in_=be_raw[:])
        bew = keep.tile([P, 1, D], F32, name="bew")
        nc.vector.tensor_copy(out=bew[:, 0, :], in_=bew_raw[:])

        E = {}
        eT = {}
        eB = {}
        GL = {}
        ST = {}
        ROWC = {}

        def front(c):
            st = {}
            thin = c >= NCH

            def widen(q):
                if q == 0:
                    st["w"] = pool.tile([P, ROWS * KV], BF16, name="wide", tag="wide", bufs=2, align_bytes=64)
                    st["xg"] = pool.tile([P, 4 * CW], BF16, name="xg", tag="xg", bufs=2, align_bytes=64)
                k = slice(KV * q, KV * (q + 1))
                nc.vector.tensor_tensor(out=st["w"][:, k], in0=raw[c][:, k].bitcast(FP8), in1=scale[:], op=ALU.mult)

            def turn(half):
                st["b%d" % half] = turn_pe(st["w"], half)

            def copy(half):
                turn_copy(st["b%d" % half], st["xg"], half, "s")

            def quant_x():
                st["xc"] = pool.tile([P, CW], U32, name="xc", tag="xc", bufs=2, align_bytes=64)
                st["xs"] = pool.tile([P, CW], U8, name="xs", tag="xs", bufs=2, align_bytes=64)
                nc.vector.quantize_mx(out=st["xc"][:].bitcast(FP8X4), scales=st["xs"][:], in_=st["xg"][:])

            def stage1(q):
                b = front_bank()
                r = slice(P * q, P * (q + 1))
                for t in range(4):
                    m = slice(P * t, P * (t + 1))
                    nc.tensor.matmul_mx(
                        out=b[:, m], lhsT=wc[:, m].bitcast(FP8X4), lhsT_scale=ws[:, m],
                        rhs=st["xc"][:, r].bitcast(FP8X4), rhs_scale=st["xs"][:, r], start=True, stop=True,
                    )
                st["h%d" % q] = b

            def hidden(q):
                if q == 0:
                    st["hg"] = pool.tile([P, 4 * CW], BF16, name="hg", tag="hg", bufs=2, align_bytes=64)
                nc.vector.tensor_tensor(
                    out=st["hg"][:, 512 * q : 512 * (q + 1)].rearrange("p (r t) -> p r t", t=4),
                    in0=st["h%d" % q][:].rearrange("p (t r) -> p r t", t=4),
                    in1=bh[:].to_broadcast([P, P, 4]),
                    op=ALU.add,
                )

            def quant_h():
                st["hc"] = pool.tile([P, CW], U32, name="hc", tag="hc", bufs=2, align_bytes=64)
                st["hs"] = pool.tile([P, CW], U8, name="hs", tag="hs", bufs=2, align_bytes=64)
                nc.vector.quantize_mx(out=st["hc"][:].bitcast(FP8X4), scales=st["hs"][:], in_=st["hg"][:])

            def stage2():
                b = front_bank()
                if thin:
                    nc.tensor.matmul_mx(
                        out=b[:], lhsT=wec[:].bitcast(FP8X4), lhsT_scale=wes[:],
                        rhs=st["hc"][:].bitcast(FP8X4), rhs_scale=st["hs"][:], start=True, stop=True,
                    )
                else:
                    for q in range(ROWS):
                        r = slice(P * q, P * (q + 1))
                        nc.tensor.matmul_mx(
                            out=b[:, r], lhsT=st["hc"][:, r].bitcast(FP8X4), lhsT_scale=st["hs"][:, r],
                            rhs=wec[:].bitcast(FP8X4), rhs_scale=wes[:], start=True, stop=True,
                        )
                st["e"] = b

            def ecopy():
                if thin:
                    t = pool.tile([P, CW], F32, name="eT", tag="eT", bufs=2)
                    nc.scalar.activation(out=t[:], in_=st["e"][:], func=ACT.Identity, bias=be[:])
                    eT[c] = t
                    h = pool.tile([P, CW], BF16, name="eB", tag="eB", bufs=2)
                    nc.scalar.activation(out=h[:], in_=st["e"][:], func=ACT.Identity, bias=be[:])
                    eB[c] = h
                else:
                    t = pool.tile([P, CW], F32, name="E", tag="E", bufs=2)
                    nc.vector.tensor_tensor(
                        out=t[:].rearrange("p (q d) -> p q d", d=D), in0=st["e"][:].rearrange("p (q d) -> p q d", d=D),
                        in1=bew[:].to_broadcast([P, ROWS, D]), op=ALU.add,
                    )
                    E[c] = t
                    st["eb"] = t

            def eback():
                if thin:
                    b = front_bank()
                    for q in range(ROWS):
                        r = slice(P * q, P * (q + 1))
                        nc.tensor.transpose(b[:, r], eT[c][:, r], ident[:])
                    st["eb"] = b

            def split_b():
                if thin:
                    g = pool.tile([P, 2, CW], BF16, name="GL", tag="GL", bufs=2)
                    d = pool.tile([P, CW], BF16, name="dl", tag="dl", bufs=2)
                    nc.vector.scalar_tensor_tensor(
                        out=d[:], in0=eT[c][:], scalar=-1.0, in1=eB[c][:], op0=ALU.mult, op1=ALU.add
                    )
                    nc.vector.tensor_scalar(out=g[:, 0, :], in0=eB[c][:], scalar1=-1.0, scalar2=None, op0=ALU.mult)
                    nc.vector.tensor_scalar(out=g[:, 1, :], in0=d[:], scalar1=2.0, scalar2=None, op0=ALU.mult)
                    GL[c] = g

            def rows_a():
                t = pool.tile([P, CW], F32, name="xp", tag="xp", bufs=2)
                nc.vector.tensor_tensor(out=t[:], in0=pp[:, CW * c : CW * (c + 1)], in1=st["eb"][:], op=ALU.subtract)
                st["xp"] = t
                s = pool.tile([P, ROWS, NNEG + 1], F32, name="ST", tag="ST", bufs=4)
                ST[c] = s
                if not thin:
                    h = pool.tile([P, CW], BF16, name="er", tag="er", bufs=2)
                    nc.scalar.copy(out=h[:], in_=E[c][:])
                    st["er"] = h

            def square_sums(src, dst):
                for q in range(ROWS):
                    junk = pool.tile([P, P], BF16, name="junk", tag="junk", bufs=4)
                    nc.scalar.activation(out=junk[:], in_=src[:, P * q : P * (q + 1)], func=ACT.Square, accum_out=dst[q])

            def rows_b():
                x = st["xp"]
                nc.vector.tensor_scalar(out=x[:], in0=x[:], scalar1=0.0, scalar2=None, op0=ALU.max)
                r = pool.tile([P, ROWS], F32, name="rowc", tag="rowc", bufs=4)
                ROWC[c] = r
                cols = [r[:, q : q + 1] for q in range(ROWS)]
                if thin:
                    square_sums(st["eb"], cols)
                else:
                    d = pool.tile([P, CW], F32, name="ed", tag="ed", bufs=2)
                    nc.vector.tensor_tensor(out=d[:], in0=st["er"][:], in1=E[c][:], op=ALU.subtract)
                    st["ed"] = d

            def rows_c():
                if not thin:
                    r = ROWC[c]
                    square_sums(st["ed"], [r[:, q : q + 1] for q in range(ROWS)])
                square_sums(st["xp"], [ST[c][:, q, 0:1] for q in range(ROWS)])

            def rows_d():
                if not thin:
                    nc.vector.tensor_scalar(out=ROWC[c][:], in0=ROWC[c][:], scalar1=-1.0, scalar2=None, op0=ALU.mult)

            return [
                [lambda: widen(0)],
                [lambda: widen(1)],
                [lambda: turn(0), lambda: widen(2)],
                [lambda: copy(0), lambda: widen(3)],
                [lambda: turn(1)],
                [lambda: copy(1)],
                [quant_x],
                [lambda: stage1(0)],
                [lambda: hidden(0), lambda: stage1(1)],
                [lambda: hidden(1), lambda: stage1(2)],
                [lambda: hidden(2), lambda: stage1(3)],
                [lambda: hidden(3)],
                [quant_h],
                [stage2],
                [ecopy],
                [eback],
                [rows_a],
                [rows_b, split_b],
                [rows_c],
                [rows_d],
            ]

        def run(piece):
            for fn in piece:
                fn()

        fd = front(0)
        fm = front(4)
        for i in range(len(fd)):
            run(fd[i])
            if i < 10:
                spread(6 + i)
            run(fm[i])
        for c in order[2:]:
            load_raw(c)

        pieces = {}
        for x in range(1, 4):
            for c in (x, x + 4):
                for i, piece in enumerate(front(c)):
                    pieces.setdefault(32 * x - 31 + 29 * i // 20, []).extend(piece)

        due = {}

        def later(s, fn):
            due.setdefault(s, []).append(fn)

        NG = 2048 // G
        TG = 128 // G
        CG = 4 * TG
        JG = NNEG // CG
        MD = {}
        SD = {}
        MI = {}
        MJ = {}
        ACC = {}
        UB = {}
        RB = {}

        def planes(g):
            tile = g // TG
            c = tile // 4
            d0 = G * (g % TG)
            k = g // (2 * TG)
            cm = NCH + k // 2
            i0 = 256 * (k % 2) + G * (g % (2 * TG))
            j0 = JG * (g % CG)
            md = pool.tile([P, G, NNEG], BF16, name="md", tag="md", bufs=3)
            sd = pool.tile([P, G, NNEG], F32, name="sd", tag="sd", bufs=4)
            mi = pool.tile([P, G, NNEG], BF16, name="mi", tag="mi", bufs=4)
            mj = pool.tile([P, JG, CW], BF16, name="mj", tag="mj", bufs=4)
            MD[g] = md
            SD[g] = sd
            MI[g] = mi
            MJ[g] = mj
            col = D * (tile % 4) + d0
            for x in range(G):
                nc.vector.tensor_scalar(
                    out=md[:, x, :], in0=NB[:, d0 + x, :], scalar1=E[c][:, col + x : col + x + 1], scalar2=None, op0=ALU.max
                )
                nc.scalar.activation(
                    out=sd[:, x, :], in_=md[:, x, :], func=ACT.Square, bias=E[c][:, col + x : col + x + 1], scale=-1.0
                )
                nc.vector.tensor_scalar(
                    out=mi[:, x, :], in0=nT[:], scalar1=eT[cm][:, i0 + x : i0 + x + 1], scalar2=None, op0=ALU.max
                )
                if x % 4 == 3:
                    y = x // 4
                    nc.vector.tensor_scalar(
                        out=mj[:, y, :], in0=eB[cm][:], scalar1=nTf[:, j0 + y : j0 + y + 1], scalar2=None, op0=ALU.max
                    )

        SP = {}

        def pair_adds(g):
            sp = pool.tile([P, PAIRS, NNEG], F32, name="sp", tag="sp", bufs=3)
            nc.vector.tensor_tensor(
                out=sp[:], in0=SD[g][:, 0:PAIRS, :], in1=SD[g][:, PAIRS : 2 * PAIRS, :], op=ALU.add
            )
            SP[g] = sp

        def adds(g, s):
            tile = g // TG
            if g % TG == 0:
                ACC[tile] = bank("acc", 2)
            blocks = [SP[g][:, x, :] for x in range(PAIRS)] + [SD[g][:, x, :] for x in range(2 * PAIRS, G)]
            for x in range(len(blocks)):
                nc.tensor.matmul(
                    ACC[tile][:, 0:P], lhsT=blocks[x], rhs=ident[:], is_transpose=True,
                    start=(g % TG == 0 and x == 0), stop=(g % TG == TG - 1 and x == len(blocks) - 1),
                )
            if g % TG == TG - 1:
                finish_direct(tile, s)

        def finish_direct(tile, s):
            c = tile // 4
            q = tile % 4
            cell = {}

            def f0():
                t = pool.tile([P, P], F32, name="us", tag="us", bufs=3)
                nc.scalar.copy(out=t[:], in_=ACC[tile][:, 0:P])
                cell["t"] = t

            def f1():
                nc.tensor.transpose(ACC[tile][:, P : 2 * P], cell["t"][:], ident[:])

            def f2():
                nc.scalar.activation(
                    out=ST[c][:, q, 1 : NNEG + 1], in_=ACC[tile][:, P : 2 * P], func=ACT.Relu, bias=ROWC[c][:, q : q + 1]
                )

            later(s + 2, f0)
            later(s + 3, f1)
            later(s + 4, f2)
            if q % 2:
                store(c, q // 2, s + 5)

        def store(c, h, s):
            cell = {}

            def f0():
                o = pool.tile([P, 2, NNEG + 1], F32, name="om", tag="om", bufs=3)
                nc.scalar.activation(out=o[:], in_=ST[c][:, 2 * h : 2 * h + 2, :], func=ACT.Sqrt)
                cell["o"] = o

            def f1():
                o = cell["o"]
                nc.vector.tensor_scalar(out=o[:], in0=o[:], scalar1=-1.0, scalar2=None, op0=ALU.mult)
                t0 = ROWS * c + 2 * h
                nc.sync.dma_start(out=out_view[:, t0 : t0 + 2, :], in_=o[:])

            later(s, f0)
            later(s + 1, f1)

        def thins_i(g, s):
            k = g // (2 * TG)
            cm = NCH + k // 2
            u = (g % (2 * TG)) // TG
            q = 2 * (k % 2) + u
            if g % TG == 0:
                UB[g // TG] = bank("U", 2)
            ub = UB[g // TG]
            for x in range(G):
                i = G * (g % TG) + x
                nc.tensor.matmul(
                    ub[:, 2 * i : 2 * i + 2], lhsT=MI[g][:, x, :], rhs=GL[cm][:, :, P * q + i], start=True, stop=True
                )
            if g % TG == TG - 1:
                nc.tensor.matmul(
                    ub[:, 256:384], lhsT=nT[:], rhs=GL[cm][:, 0, P * q : P * (q + 1)], start=True, stop=True
                )
                finish_u(k, u, g // TG, s)

        def thins_j(g, s):
            m = g // CG
            if g % CG == 0:
                RB[m] = bank("R", 2)
            rb = RB[m]
            for x in range(JG):
                j = JG * (g % CG) + x
                for v in range(ROWS):
                    nc.tensor.matmul(
                        rb[:, P * v + j : P * v + j + 1], lhsT=MJ[g][:, x, P * v : P * (v + 1)], rhs=nT[:, j : j + 1],
                        start=True, stop=True,
                    )
            if g % CG == CG - 1:
                finish_r(m, s)

        UT = {}

        def finish_u(k, u, key, s):
            cm = NCH + k // 2
            q = 2 * (k % 2) + u
            cell = {}

            def f0():
                t = pool.tile([P, P], F32, name="u0", tag="u0", bufs=2)
                nc.vector.tensor_reduce(
                    out=t[:], in_=UB[key][:, 0:256].rearrange("p (i a) -> p i a", a=2), axis=AX.X, op=ALU.add
                )
                t2 = pool.tile([P, P], F32, name="us", tag="us", bufs=3)
                nc.vector.tensor_tensor(out=t2[:], in0=UB[key][:, 256:384], in1=t[:], op=ALU.add)
                cell["t"] = t2

            def f1():
                nc.tensor.transpose(UB[key][:, 384:512], cell["t"][:], ident[:])

            def f2():
                t1 = pool.tile([P, P], F32, name="t1", tag="t1", bufs=6)
                nc.scalar.activation(out=t1[:], in_=UB[key][:, 384:512], func=ACT.Identity, bias=ROWC[cm][:, q : q + 1])
                UT[key] = t1

            later(s + 2, f0)
            later(s + 3, f1)
            later(s + 4, f2)

        def finish_r(m, s):
            cm = NCH + m

            def f0():
                for q in range(ROWS):
                    nc.vector.tensor_tensor(
                        out=ST[cm][:, q, 1 : NNEG + 1], in0=RB[m][:, P * q : P * (q + 1)], in1=UT[ROWS * m + q][:],
                        op=ALU.add,
                    )

            def f1():
                nc.vector.tensor_scalar(out=ST[cm][:], in0=ST[cm][:], scalar1=0.0, scalar2=None, op0=ALU.max)

            later(s + 5, f0)
            later(s + 6, f1)
            store(cm, 0, s + 7)
            store(cm, 1, s + 7)

        for s in range(NG + 12):
            for fn in due.get(s, []):
                fn()
            run(pieces.get(s, []))
            if s < NG:
                planes(s)
            if 1 <= s <= NG:
                pair_adds(s - 1)
            if s % 2 and 2 <= s <= NG + 1:
                adds(s - 2, s)
            if 1 <= s <= NG:
                thins_i(s - 1, s)
                thins_j(s - 1, s)
            if s % 2 == 0 and 2 <= s <= NG + 1:
                adds(s - 2, s)
